import numpy as np
import ml_dtypes


def mxq(x, axis, fmt="e4m3"):
    dtype, down = {"e4m3": (ml_dtypes.float8_e4m3fn, 7), "e5m2": (ml_dtypes.float8_e5m2, 14)}[fmt]
    v = np.moveaxis(np.asarray(x, np.float32).astype(ml_dtypes.bfloat16).astype(np.float64), axis, -1)
    blocks = v.reshape(v.shape[:-1] + (-1, 32))
    amax = np.abs(blocks).max(-1, keepdims=True)
    byte = np.maximum(np.where(amax > 0, np.frexp(amax)[1] - 1 + 127, 0) - down, 1)
    scale = np.exp2(byte - 127.0)
    codes = (blocks / scale).astype(np.float32).astype(dtype).astype(np.float64)
    return np.moveaxis((codes * scale).reshape(v.shape), -1, axis)


WIDE = False


def mx_kscale(k):
    if not WIDE:
        return np.ones(k)
    levels = np.array([10, -10, 5, -5, 0])
    a = np.random.permutation(np.resize(levels, k // 512 * 4)).reshape(k // 512, 4)
    idx = np.arange(k)
    return np.exp2(a[idx // 512, idx % 128 // 32])


BF16 = ml_dtypes.bfloat16


def bf(x):
    return np.asarray(x, np.float32).astype(BF16)


def f64(x):
    return np.asarray(x).astype(np.float64)


N, C, D, H, W, GD, GH, GW, FD, FH, FW = 2, 512, 16, 16, 16, 8, 8, 8, 4, 8, 8
V = D * H * W
G = GD * GH * GW
PD, PH, PW = D // GD, H // GH, W // GW


def erf(z):
    a = np.minimum(np.abs(z), 6.0)
    q = 2.0 * a * a
    t = a.copy()
    s = a.copy()
    n = 0
    while np.any(t > 1e-18 * s):
        n += 1
        t = t * q / (2 * n + 1)
        s = s + t
    return np.sign(z) * (2.0 / np.sqrt(np.pi)) * np.exp(-a * a) * s


def gelu(t):
    return 0.5 * t * (1.0 + erf(t / np.sqrt(2.0)))


def block(t, ps):
    n, c, d, h, w = t.shape
    t = t.reshape(n, c, d // ps[0], ps[0], h // ps[1], ps[1], w // ps[2], ps[2])
    return t.transpose(0, 1, 2, 4, 6, 3, 5, 7).reshape(n, c, -1, ps[0] * ps[1] * ps[2])


def unblock(t, gs, ps):
    n, c = t.shape[:2]
    t = t.reshape(n, c, gs[0], gs[1], gs[2], ps[0], ps[1], ps[2]).transpose(0, 1, 2, 5, 3, 6, 4, 7)
    return t.reshape(n, c, gs[0] * ps[0], gs[1] * ps[1], gs[2] * ps[2])


def setup_inputs():
    s = mx_kscale(C)
    return {"x_norm": bf(np.random.standard_normal((N, C, D, H, W)) * s[None, :, None, None, None]),
            "w1_u": bf(np.random.standard_normal((C, C)) / np.sqrt(C) / s[None, :]),
            "b1_u": bf(np.random.standard_normal(C) * 0.3),
            "w2": bf(np.random.standard_normal((G, G)) / np.sqrt(G)),
            "b2": bf(np.random.standard_normal(G) * 0.3)}


def reference(x_norm, w1_u, b1_u, w2, b2):
    z = mxq(f64(w1_u), 1, "e4m3") @ mxq(f64(x_norm).reshape(N, C, V), 1, "e4m3")
    u = gelu(z + f64(b1_u)[None, :, None]).reshape(N, C, D, H, W)
    u = block(u, (PD, PH, PW))
    y = (mxq(f64(w2), 1, "e4m3") @ mxq(u, 2, "e4m3")) + f64(b2)[None, None, :, None]
    return unblock(y, (GD, GH, GW), (PD, PH, PW))

@@ -1,0 +1,202 @@
+from contextlib import ExitStack
+
+import concourse.mybir as mybir
+from concourse.masks import make_identity
+
+F32 = mybir.dt.float32
+BF16 = mybir.dt.bfloat16
+U32 = mybir.dt.uint32
+U8 = mybir.dt.uint8
+FP8X4 = mybir.dt.float8_e4m3fn_x4
+GELU = mybir.ActivationFunctionType.Gelu
+ADD = mybir.AluOpType.add
+
+P = 128
+PACK = 4
+BATCH = 2
+CHANNELS = 512
+SIDE = 16
+VOXELS = SIDE * SIDE * SIDE
+CELLS = 512
+GRID = 8
+PLANE = SIDE * SIDE
+BLOCKS = CHANNELS // P
+CHUNK = 4 * PLANE
+CHUNKS = VOXELS // CHUNK
+HALF = CELLS // 2
+
+FLOPS = 2 * 2 * BATCH * CHANNELS * CHANNELS * VOXELS
+
+
+def transpose_and_quantise(nc, grouped_pool, flipped_pool, identity, source, codes, scales):
+    words = source.bitcast(F32)
+    grouped = grouped_pool.tile([P, BLOCKS * P * PACK], BF16, align_bytes=64)
+    grouped_words = grouped[:].bitcast(F32).rearrange("p (b r u) -> p b r u", b=BLOCKS, r=P, u=2)
+    for pair in range(BLOCKS // 2):
+        flipped = flipped_pool.tile([P, 2, 2, P], F32, tag="flipped")
+        for b in range(2):
+            for u in range(2):
+                first = ((2 * pair + b) * 2 + u) * P
+                nc.tensor.transpose(flipped[:, b, u, :], words[:, first : first + P], identity)
+        nc.scalar.copy(
+            out=grouped_words[:, 2 * pair : 2 * pair + 2],
+            in_=flipped[:].rearrange("p b u r -> p b r u"),
+        )
+    nc.vector.quantize_mx(out=codes.bitcast(FP8X4), scales=scales, in_=grouped[:])
+
+
+def tile_getspatialgatingweights_pa_t_kernel(tc, x_norm, w1_u, b1_u, w2, b2, out):
+    nc = tc.nc
+    x_flat = x_norm.rearrange("n c d h w -> n c (d h w)")
+    out_flat = out.rearrange("n c d h w -> n c (d h w)")
+
+    with ExitStack() as stack:
+        keep = stack.enter_context(tc.tile_pool(name="keep", bufs=1))
+        raw_pool = stack.enter_context(tc.tile_pool(name="raw", bufs=CHUNKS))
+        x_grouped_pool = stack.enter_context(tc.tile_pool(name="x_grouped", bufs=2))
+        u_pool = stack.enter_context(tc.tile_pool(name="u", bufs=8))
+        grouped_pool = stack.enter_context(tc.tile_pool(name="grouped", bufs=3))
+        u_mx_pool = stack.enter_context(tc.tile_pool(name="u_mx", bufs=3))
+        result_pool = stack.enter_context(tc.tile_pool(name="result", bufs=3))
+        z_pool = stack.enter_context(tc.psum_pool(name="z", bufs=3))
+        flipped_pool = stack.enter_context(tc.psum_pool(name="flipped", bufs=2))
+        y_pool = stack.enter_context(tc.psum_pool(name="y", bufs=3))
+
+        identity = keep.tile([P, P], F32)
+        make_identity(nc, identity[:])
+
+        def load_weight(weight):
+            rows = u_pool.tile([P, BLOCKS * CHANNELS], BF16, tag="u")
+            nc.sync.dma_start(
+                out=rows[:].rearrange("r (b k) -> r b k", b=BLOCKS),
+                in_=weight.rearrange("(b r) k -> r b k", r=P),
+            )
+            return rows
+
+        def load_chunk(n, chunk):
+            raw = raw_pool.tile([P, PACK, CHUNK], BF16)
+            channels = x_flat[n].rearrange("(u p e) v -> u p e v", u=2, p=P, e=2)
+            for u in range(2):
+                nc.sync.dma_start(
+                    out=raw[:, 2 * u : 2 * u + 2, :],
+                    in_=channels[u][:, :, chunk * CHUNK : (chunk + 1) * CHUNK],
+                )
+            return raw
+
+        def quantise_chunk(raw, codes, scales):
+            x_grouped = x_grouped_pool.tile([P, CHUNK * PACK], BF16, align_bytes=64)
+            nc.vector.tensor_copy(
+                out=x_grouped[:].rearrange("p (r pw gw t) -> p r pw gw t", pw=2, gw=GRID, t=PACK),
+                in_=raw[:].rearrange("p t (r gw pw) -> p r pw gw t", gw=GRID, pw=2),
+            )
+            nc.vector.quantize_mx(out=codes.bitcast(FP8X4), scales=scales, in_=x_grouped[:])
+
+        b1_rows = keep.tile([P, P], BF16)
+        nc.vector.memset(b1_rows[:], 0.0)
+        nc.sync.dma_start(out=b1_rows[0:BLOCKS, :], in_=b1_u.rearrange("(b r) -> b r", r=P))
+        w1_rows = load_weight(w1_u)
+        raw_chunks = [load_chunk(0, chunk) for chunk in range(CHUNKS)]
+        w2_rows = load_weight(w2)
+        b2_bf16 = keep.tile([P, CELLS], BF16)
+        nc.sync.dma_start(out=b2_bf16[:], in_=b2.partition_broadcast(P))
+
+        b1_rows_f32 = keep.tile([P, P], F32)
+        nc.vector.tensor_copy(out=b1_rows_f32[:], in_=b1_rows[:])
+        b1_flipped = flipped_pool.tile([P, 2, 2, P], F32, tag="flipped")
+        nc.tensor.transpose(b1_flipped[:, 0, 0, :], b1_rows_f32[:], identity[:])
+        b1_columns = keep.tile([P, BLOCKS], F32)
+        nc.vector.tensor_copy(out=b1_columns[:], in_=b1_flipped[:, 0, 0, 0:BLOCKS])
+
+        w1_codes = keep.tile([P, CHANNELS], U32, align_bytes=64)
+        w1_scales = keep.tile([P, CHANNELS], U8, align_bytes=64)
+        transpose_and_quantise(
+            nc, grouped_pool, flipped_pool, identity[:], w1_rows[:], w1_codes[:], w1_scales[:]
+        )
+
+        x_codes = [keep.tile([P, VOXELS], U32, align_bytes=64, name="x_codes%d" % n) for n in range(BATCH)]
+        x_scales = [keep.tile([P, VOXELS], U8, align_bytes=64, name="x_scales%d" % n) for n in range(BATCH)]
+
+        def quantise_volume_chunk(n, chunk, raw):
+            columns = slice(chunk * CHUNK, (chunk + 1) * CHUNK)
+            quantise_chunk(raw, x_codes[n][:, columns], x_scales[n][:, columns])
+
+        for chunk in range(CHUNKS):
+            quantise_volume_chunk(0, chunk, raw_chunks[chunk])
+
+        w2_codes = keep.tile([P, CELLS], U32, align_bytes=64)
+        w2_scales = keep.tile([P, CELLS], U8, align_bytes=64)
+        transpose_and_quantise(
+            nc, grouped_pool, flipped_pool, identity[:], w2_rows[:], w2_codes[:], w2_scales[:]
+        )
+        b2_all = keep.tile([P, CELLS], F32)
+        nc.vector.tensor_copy(out=b2_all[:], in_=b2_bf16[:])
+
+        for n in range(BATCH):
+            if n + 1 < BATCH:
+                raw_chunks = [load_chunk(n + 1, chunk) for chunk in range(CHUNKS)]
+            for block in range(BLOCKS):
+                if n + 1 < BATCH:
+                    quantise_volume_chunk(n + 1, block, raw_chunks[block])
+                channels = slice(block * P, (block + 1) * P)
+                result = result_pool.tile([P, VOXELS], F32)
+                result_view = result[:].rearrange(
+                    "c (gd pd gh ph gw pw) -> c pd ph gd gh gw pw", gd=GRID, pd=2, gh=GRID, ph=2, gw=GRID, pw=2
+                )
+                for pd in range(2):
+                    u = u_pool.tile([P, 4 * CELLS], BF16, tag="u")
+                    u_view = u[:].rearrange("c (q g) -> c q g", q=4)
+                    for pair in range(GRID // 2):
+                        z = z_pool.tile([P, 2, PLANE], F32)
+                        for i in range(2):
+                            d = 2 * (2 * pair + i) + pd
+                            plane = slice(d * PLANE, (d + 1) * PLANE)
+                            nc.tensor.matmul_mx(
+                                out=z[:, i, :],
+                                lhsT=w1_codes[:, channels].bitcast(FP8X4),
+                                lhsT_scale=w1_scales[:, channels],
+                                rhs=x_codes[n][:, plane].bitcast(FP8X4),
+                                rhs_scale=x_scales[n][:, plane],
+                                start=True,
+                                stop=True,
+                            )
+                        nc.scalar.activation(
+                            out=u_view[:, :, pair * P : (pair + 1) * P].rearrange("c q (a gw) -> c q a gw", gw=GRID),
+                            in_=z[:].rearrange("c i (gh q gw) -> c q (i gh) gw", q=4, gw=GRID),
+                            func=GELU,
+                            bias=b1_columns[:, block : block + 1],
+                            scale=1.0,
+                        )
+
+                    u_codes = u_mx_pool.tile([P, 4 * P], U32, align_bytes=64)
+                    u_scales = u_mx_pool.tile([P, 4 * P], U8, align_bytes=64)
+                    transpose_and_quantise(
+                        nc, grouped_pool, flipped_pool, identity[:], u[:], u_codes[:], u_scales[:]
+                    )
+
+                    for half in range(2):
+                        cells = slice(half * HALF, (half + 1) * HALF)
+                        for ph in range(2):
+                            y = y_pool.tile([P, 2, HALF], F32)
+                            for pw in range(2):
+                                place = slice((2 * ph + pw) * P, (2 * ph + pw + 1) * P)
+                                nc.tensor.matmul_mx(
+                                    out=y[:, pw, :],
+                                    lhsT=u_codes[:, place].bitcast(FP8X4),
+                                    lhsT_scale=u_scales[:, place],
+                                    rhs=w2_codes[:, cells].bitcast(FP8X4),
+                                    rhs_scale=w2_scales[:, cells],
+                                    start=True,
+                                    stop=True,
+                                )
+                            nc.vector.tensor_tensor(
+                                out=result_view[:, pd, ph, half * 4 : (half + 1) * 4],
+                                in0=y[:].rearrange("c pw (gd gh gw) -> c gd gh gw pw", gd=4, gh=GRID),
+                                in1=b2_all[:, cells]
+                                .rearrange("c (gd gh gw) -> c gd gh gw", gd=4, gh=GRID)
+                                .unsqueeze(4)
+                                .to_broadcast([P, 4, GRID, GRID, 2]),
+                                op=ADD,
+                            )
+                for half in range(2):
+                    voxels = slice(half * (VOXELS // 2), (half + 1) * (VOXELS // 2))
+                    nc.sync.dma_start(out=out_flat[n, channels, voxels], in_=result[:, voxels])

@@ -21,28 +21,16 @@ CELLS = 512
 GRID = 8
 PLANE = SIDE * SIDE
 BLOCKS = CHANNELS // P
+PIECES = BATCH * BLOCKS * 2
 CHUNK = 4 * PLANE
 CHUNKS = VOXELS // CHUNK
+SLAB = 2 * PLANE
+SLABS = VOXELS // SLAB
+SLAB_ROWS = SLAB // SIDE
+VECTOR_ROWS = 20
 HALF = CELLS // 2
 
 FLOPS = 2 * 2 * BATCH * CHANNELS * CHANNELS * VOXELS
-
-
-def transpose_and_quantise(nc, grouped_pool, flipped_pool, identity, source, codes, scales):
-    words = source.bitcast(F32)
-    grouped = grouped_pool.tile([P, BLOCKS * P * PACK], BF16, align_bytes=64)
-    grouped_words = grouped[:].bitcast(F32).rearrange("p (b r u) -> p b r u", b=BLOCKS, r=P, u=2)
-    for pair in range(BLOCKS // 2):
-        flipped = flipped_pool.tile([P, 2, 2, P], F32, tag="flipped")
-        for b in range(2):
-            for u in range(2):
-                first = ((2 * pair + b) * 2 + u) * P
-                nc.tensor.transpose(flipped[:, b, u, :], words[:, first : first + P], identity)
-        nc.scalar.copy(
-            out=grouped_words[:, 2 * pair : 2 * pair + 2],
-            in_=flipped[:].rearrange("p b u r -> p b r u"),
-        )
-    nc.vector.quantize_mx(out=codes.bitcast(FP8X4), scales=scales, in_=grouped[:])
 
 
 def tile_getspatialgatingweights_pa_t_kernel(tc, x_norm, w1_u, b1_u, w2, b2, out):
@@ -53,7 +41,7 @@ def tile_getspatialgatingweights_pa_t_kernel(tc, x_norm, w1_u, b1_u, w2, b2, out
     with ExitStack() as stack:
         keep = stack.enter_context(tc.tile_pool(name="keep", bufs=1))
         raw_pool = stack.enter_context(tc.tile_pool(name="raw", bufs=CHUNKS))
-        x_grouped_pool = stack.enter_context(tc.tile_pool(name="x_grouped", bufs=2))
+        x_grouped_pool = stack.enter_context(tc.tile_pool(name="x_grouped", bufs=3))
         u_pool = stack.enter_context(tc.tile_pool(name="u", bufs=8))
         grouped_pool = stack.enter_context(tc.tile_pool(name="grouped", bufs=3))
         u_mx_pool = stack.enter_context(tc.tile_pool(name="u_mx", bufs=3))
@@ -64,6 +52,13 @@ def tile_getspatialgatingweights_pa_t_kernel(tc, x_norm, w1_u, b1_u, w2, b2, out
 
         identity = keep.tile([P, P], F32)
         make_identity(nc, identity[:])
+
+        x_codes = [keep.tile([P, VOXELS], U32, align_bytes=64, name="x_codes%d" % n) for n in range(BATCH)]
+        x_scales = [keep.tile([P, VOXELS], U8, align_bytes=64, name="x_scales%d" % n) for n in range(BATCH)]
+        w1_codes = keep.tile([P, CHANNELS], U32, align_bytes=64)
+        w1_scales = keep.tile([P, CHANNELS], U8, align_bytes=64)
+        w2_codes = keep.tile([P, CELLS], U32, align_bytes=64)
+        w2_scales = keep.tile([P, CELLS], U8, align_bytes=64)
 
         def load_weight(weight):
             rows = u_pool.tile([P, BLOCKS * CHANNELS], BF16, tag="u")
@@ -83,13 +78,105 @@ def tile_getspatialgatingweights_pa_t_kernel(tc, x_norm, w1_u, b1_u, w2, b2, out
                 )
             return raw
 
-        def quantise_chunk(raw, codes, scales):
-            x_grouped = x_grouped_pool.tile([P, CHUNK * PACK], BF16, align_bytes=64)
-            nc.vector.tensor_copy(
-                out=x_grouped[:].rearrange("p (r pw gw t) -> p r pw gw t", pw=2, gw=GRID, t=PACK),
-                in_=raw[:].rearrange("p t (r gw pw) -> p r pw gw t", gw=GRID, pw=2),
+        def regroup_slab(raw_chunks, slab):
+            chunk, part = divmod(slab, CHUNK // SLAB)
+            x_grouped = x_grouped_pool.tile([P, SLAB * PACK], BF16, align_bytes=64)
+            source = raw_chunks[chunk][:, :, part * SLAB : (part + 1) * SLAB].rearrange(
+                "p t (r gw pw) -> p r pw gw t", gw=GRID, pw=2
             )
-            nc.vector.quantize_mx(out=codes.bitcast(FP8X4), scales=scales, in_=x_grouped[:])
+            target = x_grouped[:].rearrange("p (r pw gw t) -> p r pw gw t", pw=2, gw=GRID, t=PACK)
+            nc.vector.tensor_copy(out=target[:, 0:VECTOR_ROWS], in_=source[:, 0:VECTOR_ROWS])
+            for pw in range(2):
+                nc.scalar.copy(out=target[:, VECTOR_ROWS:SLAB_ROWS, pw], in_=source[:, VECTOR_ROWS:SLAB_ROWS, pw])
+            return x_grouped
+
+        def quantise_slab(n, slab, x_grouped):
+            columns = slice(slab * SLAB, (slab + 1) * SLAB)
+            nc.vector.quantize_mx(
+                out=x_codes[n][:, columns].bitcast(FP8X4), scales=x_scales[n][:, columns], in_=x_grouped[:]
+            )
+
+        def transpose_blocks(source):
+            words = source.bitcast(F32)
+            grouped = grouped_pool.tile([P, BLOCKS * P * PACK], BF16, align_bytes=64)
+            grouped_words = grouped[:].bitcast(F32).rearrange("p (b r u) -> p b r u", b=BLOCKS, r=P, u=2)
+            for pair in range(BLOCKS // 2):
+                flipped = flipped_pool.tile([P, 2, 2, P], F32, tag="flipped")
+                for b in range(2):
+                    for u in range(2):
+                        first = ((2 * pair + b) * 2 + u) * P
+                        nc.tensor.transpose(flipped[:, b, u, :], words[:, first : first + P], identity[:])
+                nc.scalar.copy(
+                    out=grouped_words[:, 2 * pair : 2 * pair + 2],
+                    in_=flipped[:].rearrange("p b u r -> p b r u"),
+                )
+            return grouped
+
+        def project(piece):
+            n, rest = divmod(piece, 2 * BLOCKS)
+            block, pd = divmod(rest, 2)
+            channels = slice(block * P, (block + 1) * P)
+            u = u_pool.tile([P, 4 * CELLS], BF16, tag="u")
+            u_view = u[:].rearrange("c (q g) -> c q g", q=4)
+            for pair in range(GRID // 2):
+                z = z_pool.tile([P, 2, PLANE], F32)
+                for i in range(2):
+                    d = 2 * (2 * pair + i) + pd
+                    plane = slice(d * PLANE, (d + 1) * PLANE)
+                    nc.tensor.matmul_mx(
+                        out=z[:, i, :],
+                        lhsT=w1_codes[:, channels].bitcast(FP8X4),
+                        lhsT_scale=w1_scales[:, channels],
+                        rhs=x_codes[n][:, plane].bitcast(FP8X4),
+                        rhs_scale=x_scales[n][:, plane],
+                        start=True,
+                        stop=True,
+                    )
+                nc.scalar.activation(
+                    out=u_view[:, :, pair * P : (pair + 1) * P].rearrange("c q (a gw) -> c q a gw", gw=GRID),
+                    in_=z[:].rearrange("c i (gh q gw) -> c q (i gh) gw", q=4, gw=GRID),
+                    func=GELU,
+                    bias=b1_columns[:, block : block + 1],
+                    scale=1.0,
+                )
+            return u
+
+        def mix(piece, u_codes, u_scales, result):
+            pd = piece % 2
+            result_view = result[:].rearrange(
+                "c (gd pd gh ph gw pw) -> c pd ph gd gh gw pw", gd=GRID, pd=2, gh=GRID, ph=2, gw=GRID, pw=2
+            )
+            for half in range(2):
+                cells = slice(half * HALF, (half + 1) * HALF)
+                for ph in range(2):
+                    y = y_pool.tile([P, 2, HALF], F32)
+                    for pw in range(2):
+                        place = slice((2 * ph + pw) * P, (2 * ph + pw + 1) * P)
+                        nc.tensor.matmul_mx(
+                            out=y[:, pw, :],
+                            lhsT=u_codes[:, place].bitcast(FP8X4),
+                            lhsT_scale=u_scales[:, place],
+                            rhs=w2_codes[:, cells].bitcast(FP8X4),
+                            rhs_scale=w2_scales[:, cells],
+                            start=True,
+                            stop=True,
+                        )
+                    nc.vector.tensor_tensor(
+                        out=result_view[:, pd, ph, half * 4 : (half + 1) * 4],
+                        in0=y[:].rearrange("c pw (gd gh gw) -> c gd gh gw pw", gd=4, gh=GRID),
+                        in1=b2_all[:, cells]
+                        .rearrange("c (gd gh gw) -> c gd gh gw", gd=4, gh=GRID)
+                        .unsqueeze(4)
+                        .to_broadcast([P, 4, GRID, GRID, 2]),
+                        op=ADD,
+                    )
+
+        def store(piece, result):
+            n, rest = divmod(piece, 2 * BLOCKS)
+            channels = slice((rest // 2) * P, (rest // 2 + 1) * P)
+            for half in range(2):
+                voxels = slice(half * (VOXELS // 2), (half + 1) * (VOXELS // 2))
+                nc.sync.dma_start(out=out_flat[n, channels, voxels], in_=result[:, voxels])
 
         b1_rows = keep.tile([P, P], BF16)
         nc.vector.memset(b1_rows[:], 0.0)
@@ -97,8 +184,8 @@ def tile_getspatialgatingweights_pa_t_kernel(tc, x_norm, w1_u, b1_u, w2, b2, out
         w1_rows = load_weight(w1_u)
         raw_chunks = [load_chunk(0, chunk) for chunk in range(CHUNKS)]
         w2_rows = load_weight(w2)
-        b2_bf16 = keep.tile([P, CELLS], BF16)
-        nc.sync.dma_start(out=b2_bf16[:], in_=b2.partition_broadcast(P))
+        b2_all = keep.tile([P, CELLS], BF16)
+        nc.sync.dma_start(out=b2_all[:], in_=b2.partition_broadcast(P))
 
         b1_rows_f32 = keep.tile([P, P], F32)
         nc.vector.tensor_copy(out=b1_rows_f32[:], in_=b1_rows[:])
@@ -107,96 +194,40 @@ def tile_getspatialgatingweights_pa_t_kernel(tc, x_norm, w1_u, b1_u, w2, b2, out
         b1_columns = keep.tile([P, BLOCKS], F32)
         nc.vector.tensor_copy(out=b1_columns[:], in_=b1_flipped[:, 0, 0, 0:BLOCKS])
 
-        w1_codes = keep.tile([P, CHANNELS], U32, align_bytes=64)
-        w1_scales = keep.tile([P, CHANNELS], U8, align_bytes=64)
-        transpose_and_quantise(
-            nc, grouped_pool, flipped_pool, identity[:], w1_rows[:], w1_codes[:], w1_scales[:]
-        )
+        w1_grouped = transpose_blocks(w1_rows[:])
+        waiting = regroup_slab(raw_chunks, 0)
+        nc.vector.quantize_mx(out=w1_codes[:].bitcast(FP8X4), scales=w1_scales[:], in_=w1_grouped[:])
+        for slab in range(1, SLABS):
+            x_grouped = regroup_slab(raw_chunks, slab)
+            quantise_slab(0, slab - 1, waiting)
+            waiting = x_grouped
+        quantise_slab(0, SLABS - 1, waiting)
+        raw_chunks = [load_chunk(1, chunk) for chunk in range(CHUNKS)]
 
-        x_codes = [keep.tile([P, VOXELS], U32, align_bytes=64, name="x_codes%d" % n) for n in range(BATCH)]
-        x_scales = [keep.tile([P, VOXELS], U8, align_bytes=64, name="x_scales%d" % n) for n in range(BATCH)]
-
-        def quantise_volume_chunk(n, chunk, raw):
-            columns = slice(chunk * CHUNK, (chunk + 1) * CHUNK)
-            quantise_chunk(raw, x_codes[n][:, columns], x_scales[n][:, columns])
-
-        for chunk in range(CHUNKS):
-            quantise_volume_chunk(0, chunk, raw_chunks[chunk])
-
-        w2_codes = keep.tile([P, CELLS], U32, align_bytes=64)
-        w2_scales = keep.tile([P, CELLS], U8, align_bytes=64)
-        transpose_and_quantise(
-            nc, grouped_pool, flipped_pool, identity[:], w2_rows[:], w2_codes[:], w2_scales[:]
-        )
-        b2_all = keep.tile([P, CELLS], F32)
-        nc.vector.tensor_copy(out=b2_all[:], in_=b2_bf16[:])
-
-        for n in range(BATCH):
-            if n + 1 < BATCH:
-                raw_chunks = [load_chunk(n + 1, chunk) for chunk in range(CHUNKS)]
-            for block in range(BLOCKS):
-                if n + 1 < BATCH:
-                    quantise_volume_chunk(n + 1, block, raw_chunks[block])
-                channels = slice(block * P, (block + 1) * P)
-                result = result_pool.tile([P, VOXELS], F32)
-                result_view = result[:].rearrange(
-                    "c (gd pd gh ph gw pw) -> c pd ph gd gh gw pw", gd=GRID, pd=2, gh=GRID, ph=2, gw=GRID, pw=2
-                )
-                for pd in range(2):
-                    u = u_pool.tile([P, 4 * CELLS], BF16, tag="u")
-                    u_view = u[:].rearrange("c (q g) -> c q g", q=4)
-                    for pair in range(GRID // 2):
-                        z = z_pool.tile([P, 2, PLANE], F32)
-                        for i in range(2):
-                            d = 2 * (2 * pair + i) + pd
-                            plane = slice(d * PLANE, (d + 1) * PLANE)
-                            nc.tensor.matmul_mx(
-                                out=z[:, i, :],
-                                lhsT=w1_codes[:, channels].bitcast(FP8X4),
-                                lhsT_scale=w1_scales[:, channels],
-                                rhs=x_codes[n][:, plane].bitcast(FP8X4),
-                                rhs_scale=x_scales[n][:, plane],
-                                start=True,
-                                stop=True,
-                            )
-                        nc.scalar.activation(
-                            out=u_view[:, :, pair * P : (pair + 1) * P].rearrange("c q (a gw) -> c q a gw", gw=GRID),
-                            in_=z[:].rearrange("c i (gh q gw) -> c q (i gh) gw", q=4, gw=GRID),
-                            func=GELU,
-                            bias=b1_columns[:, block : block + 1],
-                            scale=1.0,
-                        )
-
-                    u_codes = u_mx_pool.tile([P, 4 * P], U32, align_bytes=64)
-                    u_scales = u_mx_pool.tile([P, 4 * P], U8, align_bytes=64)
-                    transpose_and_quantise(
-                        nc, grouped_pool, flipped_pool, identity[:], u[:], u_codes[:], u_scales[:]
-                    )
-
-                    for half in range(2):
-                        cells = slice(half * HALF, (half + 1) * HALF)
-                        for ph in range(2):
-                            y = y_pool.tile([P, 2, HALF], F32)
-                            for pw in range(2):
-                                place = slice((2 * ph + pw) * P, (2 * ph + pw + 1) * P)
-                                nc.tensor.matmul_mx(
-                                    out=y[:, pw, :],
-                                    lhsT=u_codes[:, place].bitcast(FP8X4),
-                                    lhsT_scale=u_scales[:, place],
-                                    rhs=w2_codes[:, cells].bitcast(FP8X4),
-                                    rhs_scale=w2_scales[:, cells],
-                                    start=True,
-                                    stop=True,
-                                )
-                            nc.vector.tensor_tensor(
-                                out=result_view[:, pd, ph, half * 4 : (half + 1) * 4],
-                                in0=y[:].rearrange("c pw (gd gh gw) -> c gd gh gw pw", gd=4, gh=GRID),
-                                in1=b2_all[:, cells]
-                                .rearrange("c (gd gh gw) -> c gd gh gw", gd=4, gh=GRID)
-                                .unsqueeze(4)
-                                .to_broadcast([P, 4, GRID, GRID, 2]),
-                                op=ADD,
-                            )
-                for half in range(2):
-                    voxels = slice(half * (VOXELS // 2), (half + 1) * (VOXELS // 2))
-                    nc.sync.dma_start(out=out_flat[n, channels, voxels], in_=result[:, voxels])
+        u_tiles = {}
+        operands = {}
+        results = {}
+        for i in range(PIECES + 2):
+            if i < SLABS:
+                x_grouped = regroup_slab(raw_chunks, i)
+            if i < PIECES:
+                u_tiles[i] = project(i)
+            if i == 0:
+                w2_grouped = transpose_blocks(w2_rows[:])
+                nc.vector.quantize_mx(out=w2_codes[:].bitcast(FP8X4), scales=w2_scales[:], in_=w2_grouped[:])
+            if 1 <= i <= PIECES:
+                u_grouped = transpose_blocks(u_tiles[i - 1][:])
+            if i >= 2:
+                if i % 2 == 0:
+                    results[i // 2] = result_pool.tile([P, VOXELS], F32, name="result")
+                u_codes, u_scales = operands[i - 2]
+                mix(i - 2, u_codes, u_scales, results[i // 2])
+                if i % 2 == 1:
+                    store(i - 2, results[i // 2])
+            if 1 <= i <= PIECES:
+                u_codes = u_mx_pool.tile([P, 4 * P], U32, align_bytes=64)
+                u_scales = u_mx_pool.tile([P, 4 * P], U8, align_bytes=64)
+                nc.vector.quantize_mx(out=u_codes[:].bitcast(FP8X4), scales=u_scales[:], in_=u_grouped[:])
+                operands[i - 1] = (u_codes, u_scales)
+            if i < SLABS:
+                quantise_slab(1, i, x_grouped)

@@ -10,6 +10,7 @@ U8 = mybir.dt.uint8
 FP8X4 = mybir.dt.float8_e4m3fn_x4
 GELU = mybir.ActivationFunctionType.Gelu
 ADD = mybir.AluOpType.add
+MULT = mybir.AluOpType.mult
 
 P = 128
 PACK = 4
@@ -78,16 +79,28 @@ def tile_getspatialgatingweights_pa_t_kernel(tc, x_norm, w1_u, b1_u, w2, b2, out
                 )
             return raw
 
-        def regroup_slab(raw_chunks, slab):
+        def open_slab(raw_chunks, slab):
             chunk, part = divmod(slab, CHUNK // SLAB)
             x_grouped = x_grouped_pool.tile([P, SLAB * PACK], BF16, align_bytes=64)
             source = raw_chunks[chunk][:, :, part * SLAB : (part + 1) * SLAB].rearrange(
                 "p t (r gw pw) -> p r pw gw t", gw=GRID, pw=2
             )
             target = x_grouped[:].rearrange("p (r pw gw t) -> p r pw gw t", pw=2, gw=GRID, t=PACK)
+            return x_grouped, source, target
+
+        def regroup_slab_at_once(raw_chunks, slab):
+            x_grouped, source, target = open_slab(raw_chunks, slab)
             nc.vector.tensor_copy(out=target[:, 0:VECTOR_ROWS], in_=source[:, 0:VECTOR_ROWS])
             for pw in range(2):
                 nc.scalar.copy(out=target[:, VECTOR_ROWS:SLAB_ROWS, pw], in_=source[:, VECTOR_ROWS:SLAB_ROWS, pw])
+            return x_grouped
+
+        def regroup_slab_aside(raw_chunks, slab):
+            x_grouped, source, target = open_slab(raw_chunks, slab)
+            for pw in range(2):
+                nc.gpsimd.tensor_scalar(
+                    out=target[:, :, pw], in0=source[:, :, pw], scalar1=1.0, scalar2=0.0, op0=MULT, op1=ADD
+                )
             return x_grouped
 
         def quantise_slab(n, slab, x_grouped):
@@ -195,10 +208,10 @@ def tile_getspatialgatingweights_pa_t_kernel(tc, x_norm, w1_u, b1_u, w2, b2, out
         nc.vector.tensor_copy(out=b1_columns[:], in_=b1_flipped[:, 0, 0, 0:BLOCKS])
 
         w1_grouped = transpose_blocks(w1_rows[:])
-        waiting = regroup_slab(raw_chunks, 0)
+        waiting = regroup_slab_at_once(raw_chunks, 0)
         nc.vector.quantize_mx(out=w1_codes[:].bitcast(FP8X4), scales=w1_scales[:], in_=w1_grouped[:])
         for slab in range(1, SLABS):
-            x_grouped = regroup_slab(raw_chunks, slab)
+            x_grouped = regroup_slab_at_once(raw_chunks, slab)
             quantise_slab(0, slab - 1, waiting)
             waiting = x_grouped
         quantise_slab(0, SLABS - 1, waiting)
@@ -209,7 +222,7 @@ def tile_getspatialgatingweights_pa_t_kernel(tc, x_norm, w1_u, b1_u, w2, b2, out
         results = {}
         for i in range(PIECES + 2):
             if i < SLABS:
-                x_grouped = regroup_slab(raw_chunks, i)
+                x_grouped = regroup_slab_aside(raw_chunks, i)
             if i < PIECES:
                 u_tiles[i] = project(i)
             if i == 0:

@@ -10,7 +10,6 @@ U8 = mybir.dt.uint8
 FP8X4 = mybir.dt.float8_e4m3fn_x4
 GELU = mybir.ActivationFunctionType.Gelu
 ADD = mybir.AluOpType.add
-MULT = mybir.AluOpType.mult
 
 P = 128
 PACK = 4
@@ -30,6 +29,8 @@ SLABS = VOXELS // SLAB
 SLAB_ROWS = SLAB // SIDE
 VECTOR_ROWS = 20
 HALF = CELLS // 2
+FLIP_LAG = 2
+MIX_LAG = 4
 
 FLOPS = 2 * 2 * BATCH * CHANNELS * CHANNELS * VOXELS
 
@@ -37,19 +38,20 @@ FLOPS = 2 * 2 * BATCH * CHANNELS * CHANNELS * VOXELS
 def tile_getspatialgatingweights_pa_t_kernel(tc, x_norm, w1_u, b1_u, w2, b2, out):
     nc = tc.nc
     x_flat = x_norm.rearrange("n c d h w -> n c (d h w)")
-    out_flat = out.rearrange("n c d h w -> n c (d h w)")
+    out_planes = out.rearrange("n c (gd pd) h w -> n c pd gd (h w)", pd=2)
 
     with ExitStack() as stack:
         keep = stack.enter_context(tc.tile_pool(name="keep", bufs=1))
         raw_pool = stack.enter_context(tc.tile_pool(name="raw", bufs=CHUNKS))
         x_grouped_pool = stack.enter_context(tc.tile_pool(name="x_grouped", bufs=3))
-        u_pool = stack.enter_context(tc.tile_pool(name="u", bufs=8))
-        grouped_pool = stack.enter_context(tc.tile_pool(name="grouped", bufs=3))
-        u_mx_pool = stack.enter_context(tc.tile_pool(name="u_mx", bufs=3))
-        result_pool = stack.enter_context(tc.tile_pool(name="result", bufs=3))
+        u_pool = stack.enter_context(tc.tile_pool(name="u", bufs=4))
+        grouped_pool = stack.enter_context(tc.tile_pool(name="grouped", bufs=4))
+        u_mx_pool = stack.enter_context(tc.tile_pool(name="u_mx", bufs=4))
+        result_pool = stack.enter_context(tc.tile_pool(name="result", bufs=4))
         z_pool = stack.enter_context(tc.psum_pool(name="z", bufs=3))
         flipped_pool = stack.enter_context(tc.psum_pool(name="flipped", bufs=2))
         y_pool = stack.enter_context(tc.psum_pool(name="y", bufs=3))
+        stack.enter_context(tc.manual_schedule())
 
         identity = keep.tile([P, P], F32)
         make_identity(nc, identity[:])
@@ -79,28 +81,16 @@ def tile_getspatialgatingweights_pa_t_kernel(tc, x_norm, w1_u, b1_u, w2, b2, out
                 )
             return raw
 
-        def open_slab(raw_chunks, slab):
+        def regroup_slab(raw_chunks, slab):
             chunk, part = divmod(slab, CHUNK // SLAB)
             x_grouped = x_grouped_pool.tile([P, SLAB * PACK], BF16, align_bytes=64)
             source = raw_chunks[chunk][:, :, part * SLAB : (part + 1) * SLAB].rearrange(
                 "p t (r gw pw) -> p r pw gw t", gw=GRID, pw=2
             )
             target = x_grouped[:].rearrange("p (r pw gw t) -> p r pw gw t", pw=2, gw=GRID, t=PACK)
-            return x_grouped, source, target
-
-        def regroup_slab_at_once(raw_chunks, slab):
-            x_grouped, source, target = open_slab(raw_chunks, slab)
             nc.vector.tensor_copy(out=target[:, 0:VECTOR_ROWS], in_=source[:, 0:VECTOR_ROWS])
             for pw in range(2):
                 nc.scalar.copy(out=target[:, VECTOR_ROWS:SLAB_ROWS, pw], in_=source[:, VECTOR_ROWS:SLAB_ROWS, pw])
-            return x_grouped
-
-        def regroup_slab_aside(raw_chunks, slab):
-            x_grouped, source, target = open_slab(raw_chunks, slab)
-            for pw in range(2):
-                nc.gpsimd.tensor_scalar(
-                    out=target[:, :, pw], in0=source[:, :, pw], scalar1=1.0, scalar2=0.0, op0=MULT, op1=ADD
-                )
             return x_grouped
 
         def quantise_slab(n, slab, x_grouped):
@@ -109,87 +99,88 @@ def tile_getspatialgatingweights_pa_t_kernel(tc, x_norm, w1_u, b1_u, w2, b2, out
                 out=x_codes[n][:, columns].bitcast(FP8X4), scales=x_scales[n][:, columns], in_=x_grouped[:]
             )
 
-        def transpose_blocks(source):
+        def transpose_two_blocks(source, pair):
             words = source.bitcast(F32)
-            grouped = grouped_pool.tile([P, BLOCKS * P * PACK], BF16, align_bytes=64)
-            grouped_words = grouped[:].bitcast(F32).rearrange("p (b r u) -> p b r u", b=BLOCKS, r=P, u=2)
-            for pair in range(BLOCKS // 2):
-                flipped = flipped_pool.tile([P, 2, 2, P], F32, tag="flipped")
-                for b in range(2):
-                    for u in range(2):
-                        first = ((2 * pair + b) * 2 + u) * P
-                        nc.tensor.transpose(flipped[:, b, u, :], words[:, first : first + P], identity[:])
-                nc.scalar.copy(
-                    out=grouped_words[:, 2 * pair : 2 * pair + 2],
-                    in_=flipped[:].rearrange("p b u r -> p b r u"),
-                )
+            flipped = flipped_pool.tile([P, 2, 2, P], F32, tag="flipped")
+            for b in range(2):
+                for u in range(2):
+                    first = ((2 * pair + b) * 2 + u) * P
+                    nc.tensor.transpose(flipped[:, b, u, :], words[:, first : first + P], identity[:])
+            grouped = grouped_pool.tile([P, 2 * P * PACK], BF16, align_bytes=64)
+            nc.scalar.copy(
+                out=grouped[:].bitcast(F32).rearrange("p (b r u) -> p b r u", b=2, r=P, u=2),
+                in_=flipped[:].rearrange("p b u r -> p b r u"),
+            )
             return grouped
 
-        def project(piece):
+        def quantise_weight(rows, codes, scales):
+            halves = [transpose_two_blocks(rows[:], pair) for pair in range(2)]
+            for pair in range(2):
+                columns = slice(pair * 2 * P, (pair + 1) * 2 * P)
+                nc.vector.quantize_mx(
+                    out=codes[:, columns].bitcast(FP8X4), scales=scales[:, columns], in_=halves[pair][:]
+                )
+
+        def project(piece, u, pair):
             n, rest = divmod(piece, 2 * BLOCKS)
             block, pd = divmod(rest, 2)
             channels = slice(block * P, (block + 1) * P)
-            u = u_pool.tile([P, 4 * CELLS], BF16, tag="u")
-            u_view = u[:].rearrange("c (q g) -> c q g", q=4)
-            for pair in range(GRID // 2):
-                z = z_pool.tile([P, 2, PLANE], F32)
-                for i in range(2):
-                    d = 2 * (2 * pair + i) + pd
-                    plane = slice(d * PLANE, (d + 1) * PLANE)
-                    nc.tensor.matmul_mx(
-                        out=z[:, i, :],
-                        lhsT=w1_codes[:, channels].bitcast(FP8X4),
-                        lhsT_scale=w1_scales[:, channels],
-                        rhs=x_codes[n][:, plane].bitcast(FP8X4),
-                        rhs_scale=x_scales[n][:, plane],
-                        start=True,
-                        stop=True,
-                    )
-                nc.scalar.activation(
-                    out=u_view[:, :, pair * P : (pair + 1) * P].rearrange("c q (a gw) -> c q a gw", gw=GRID),
-                    in_=z[:].rearrange("c i (gh q gw) -> c q (i gh) gw", q=4, gw=GRID),
-                    func=GELU,
-                    bias=b1_columns[:, block : block + 1],
-                    scale=1.0,
+            z = z_pool.tile([P, 2, PLANE], F32)
+            for i in range(2):
+                d = 2 * (2 * pair + i) + pd
+                plane = slice(d * PLANE, (d + 1) * PLANE)
+                nc.tensor.matmul_mx(
+                    out=z[:, i, :],
+                    lhsT=w1_codes[:, channels].bitcast(FP8X4),
+                    lhsT_scale=w1_scales[:, channels],
+                    rhs=x_codes[n][:, plane].bitcast(FP8X4),
+                    rhs_scale=x_scales[n][:, plane],
+                    start=True,
+                    stop=True,
                 )
-            return u
+            nc.scalar.activation(
+                out=u[:]
+                .rearrange("c (q g) -> c q g", q=4)[:, :, pair * P : (pair + 1) * P]
+                .rearrange("c q (a gw) -> c q a gw", gw=GRID),
+                in_=z[:].rearrange("c i (gh q gw) -> c q (i gh) gw", q=4, gw=GRID),
+                func=GELU,
+                bias=b1_columns[:, block : block + 1],
+                scale=1.0,
+            )
 
-        def mix(piece, u_codes, u_scales, result):
-            pd = piece % 2
+        def mix(piece, ph, u_codes, u_scales, result):
+            n, rest = divmod(piece, 2 * BLOCKS)
+            block, pd = divmod(rest, 2)
             result_view = result[:].rearrange(
-                "c (gd pd gh ph gw pw) -> c pd ph gd gh gw pw", gd=GRID, pd=2, gh=GRID, ph=2, gw=GRID, pw=2
+                "c (gd gh ph gw pw) -> c ph gd gh gw pw", gd=GRID, gh=GRID, ph=2, gw=GRID, pw=2
             )
             for half in range(2):
                 cells = slice(half * HALF, (half + 1) * HALF)
-                for ph in range(2):
-                    y = y_pool.tile([P, 2, HALF], F32)
-                    for pw in range(2):
-                        place = slice((2 * ph + pw) * P, (2 * ph + pw + 1) * P)
-                        nc.tensor.matmul_mx(
-                            out=y[:, pw, :],
-                            lhsT=u_codes[:, place].bitcast(FP8X4),
-                            lhsT_scale=u_scales[:, place],
-                            rhs=w2_codes[:, cells].bitcast(FP8X4),
-                            rhs_scale=w2_scales[:, cells],
-                            start=True,
-                            stop=True,
-                        )
-                    nc.vector.tensor_tensor(
-                        out=result_view[:, pd, ph, half * 4 : (half + 1) * 4],
-                        in0=y[:].rearrange("c pw (gd gh gw) -> c gd gh gw pw", gd=4, gh=GRID),
-                        in1=b2_all[:, cells]
-                        .rearrange("c (gd gh gw) -> c gd gh gw", gd=4, gh=GRID)
-                        .unsqueeze(4)
-                        .to_broadcast([P, 4, GRID, GRID, 2]),
-                        op=ADD,
+                y = y_pool.tile([P, 2, HALF], F32)
+                for pw in range(2):
+                    nc.tensor.matmul_mx(
+                        out=y[:, pw, :],
+                        lhsT=u_codes[:, pw * P : (pw + 1) * P].bitcast(FP8X4),
+                        lhsT_scale=u_scales[:, pw * P : (pw + 1) * P],
+                        rhs=w2_codes[:, cells].bitcast(FP8X4),
+                        rhs_scale=w2_scales[:, cells],
+                        start=True,
+                        stop=True,
                     )
-
-        def store(piece, result):
-            n, rest = divmod(piece, 2 * BLOCKS)
-            channels = slice((rest // 2) * P, (rest // 2 + 1) * P)
-            for half in range(2):
-                voxels = slice(half * (VOXELS // 2), (half + 1) * (VOXELS // 2))
-                nc.sync.dma_start(out=out_flat[n, channels, voxels], in_=result[:, voxels])
+                nc.vector.tensor_tensor(
+                    out=result_view[:, ph, half * 4 : (half + 1) * 4],
+                    in0=y[:].rearrange("c pw (gd gh gw) -> c gd gh gw pw", gd=4, gh=GRID),
+                    in1=b2_all[:, cells]
+                    .rearrange("c (gd gh gw) -> c gd gh gw", gd=4, gh=GRID)
+                    .unsqueeze(4)
+                    .to_broadcast([P, 4, GRID, GRID, 2]),
+                    op=ADD,
+                )
+                if ph == 1:
+                    nc.sync.dma_start(
+                        out=out_planes[n, block * P : (block + 1) * P, pd, half * 4 : (half + 1) * 4],
+                        in_=result[:].rearrange("c (gd v) -> c gd v", gd=GRID)[:, half * 4 : (half + 1) * 4],
+                    )
 
         b1_rows = keep.tile([P, P], BF16)
         nc.vector.memset(b1_rows[:], 0.0)
@@ -207,40 +198,42 @@ def tile_getspatialgatingweights_pa_t_kernel(tc, x_norm, w1_u, b1_u, w2, b2, out
         b1_columns = keep.tile([P, BLOCKS], F32)
         nc.vector.tensor_copy(out=b1_columns[:], in_=b1_flipped[:, 0, 0, 0:BLOCKS])
 
-        w1_grouped = transpose_blocks(w1_rows[:])
-        waiting = regroup_slab_at_once(raw_chunks, 0)
-        nc.vector.quantize_mx(out=w1_codes[:].bitcast(FP8X4), scales=w1_scales[:], in_=w1_grouped[:])
+        quantise_weight(w1_rows, w1_codes, w1_scales)
+        waiting = regroup_slab(raw_chunks, 0)
         for slab in range(1, SLABS):
-            x_grouped = regroup_slab_at_once(raw_chunks, slab)
+            x_grouped = regroup_slab(raw_chunks, slab)
             quantise_slab(0, slab - 1, waiting)
             waiting = x_grouped
         quantise_slab(0, SLABS - 1, waiting)
         raw_chunks = [load_chunk(1, chunk) for chunk in range(CHUNKS)]
 
         u_tiles = {}
+        grouped_tiles = {}
         operands = {}
         results = {}
-        for i in range(PIECES + 2):
-            if i < SLABS:
-                x_grouped = regroup_slab_aside(raw_chunks, i)
-            if i < PIECES:
-                u_tiles[i] = project(i)
-            if i == 0:
-                w2_grouped = transpose_blocks(w2_rows[:])
-                nc.vector.quantize_mx(out=w2_codes[:].bitcast(FP8X4), scales=w2_scales[:], in_=w2_grouped[:])
-            if 1 <= i <= PIECES:
-                u_grouped = transpose_blocks(u_tiles[i - 1][:])
-            if i >= 2:
-                if i % 2 == 0:
-                    results[i // 2] = result_pool.tile([P, VOXELS], F32, name="result")
-                u_codes, u_scales = operands[i - 2]
-                mix(i - 2, u_codes, u_scales, results[i // 2])
-                if i % 2 == 1:
-                    store(i - 2, results[i // 2])
-            if 1 <= i <= PIECES:
-                u_codes = u_mx_pool.tile([P, 4 * P], U32, align_bytes=64)
-                u_scales = u_mx_pool.tile([P, 4 * P], U8, align_bytes=64)
-                nc.vector.quantize_mx(out=u_codes[:].bitcast(FP8X4), scales=u_scales[:], in_=u_grouped[:])
-                operands[i - 1] = (u_codes, u_scales)
-            if i < SLABS:
-                quantise_slab(1, i, x_grouped)
+        for k in range(2 * PIECES + MIX_LAG):
+            if k < 2 * SLABS and k % 2 == 0:
+                x_grouped = regroup_slab(raw_chunks, k // 2)
+            if k < 2 * PIECES:
+                if k % 2 == 0:
+                    u_tiles[k // 2] = u_pool.tile([P, 4 * CELLS], BF16, tag="u", name="u")
+                for pair in (2 * (k % 2), 2 * (k % 2) + 1):
+                    project(k // 2, u_tiles[k // 2], pair)
+            if k == 1:
+                quantise_weight(w2_rows, w2_codes, w2_scales)
+            flip = k - FLIP_LAG
+            if 0 <= flip < 2 * PIECES:
+                grouped_tiles[flip] = transpose_two_blocks(u_tiles[flip // 2][:], flip % 2)
+            mixed = k - MIX_LAG
+            if 0 <= mixed < 2 * PIECES:
+                if mixed % 2 == 0:
+                    results[mixed // 2] = result_pool.tile([P, VOXELS // 2], F32, name="result")
+                u_codes, u_scales = operands[mixed]
+                mix(mixed // 2, mixed % 2, u_codes, u_scales, results[mixed // 2])
+            if 0 <= flip < 2 * PIECES:
+                u_codes = u_mx_pool.tile([P, 2 * P], U32, align_bytes=64)
+                u_scales = u_mx_pool.tile([P, 2 * P], U8, align_bytes=64)
+                nc.vector.quantize_mx(out=u_codes[:].bitcast(FP8X4), scales=u_scales[:], in_=grouped_tiles[flip][:])
+                operands[flip] = (u_codes, u_scales)
+            if k < 2 * SLABS and k % 2 == 1:
+                quantise_slab(1, k // 2, x_grouped)

@@ -21,16 +21,22 @@ CELLS = 512
 GRID = 8
 PLANE = SIDE * SIDE
 BLOCKS = CHANNELS // P
-PIECES = BATCH * BLOCKS * 2
-CHUNK = 4 * PLANE
-CHUNKS = VOXELS // CHUNK
+PIECES = BLOCKS * 2
 SLAB = 2 * PLANE
 SLABS = VOXELS // SLAB
 SLAB_ROWS = SLAB // SIDE
-VECTOR_ROWS = 20
+CHUNK = 2 * SLAB
+CHUNKS = VOXELS // CHUNK
+BANKS = CHUNKS * PIECES
 HALF = CELLS // 2
-FLIP_LAG = 2
-MIX_LAG = 4
+FLIPS = 2 * PIECES
+FIRST_TICK = 2
+LEAD = 3
+EARLY_SLABS = 1
+SLAB_TICKS = [2 * i for i in range(SLABS - EARLY_SLABS)]
+MIX_LAG = 2
+HEAD_SCALAR_ROWS = 12
+LATE_SCALAR_ROWS = 8
 
 FLOPS = 2 * 2 * BATCH * CHANNELS * CHANNELS * VOXELS
 
@@ -42,12 +48,13 @@ def tile_getspatialgatingweights_pa_t_kernel(tc, x_norm, w1_u, b1_u, w2, b2, out
 
     with ExitStack() as stack:
         keep = stack.enter_context(tc.tile_pool(name="keep", bufs=1))
-        raw_pool = stack.enter_context(tc.tile_pool(name="raw", bufs=CHUNKS))
+        weight_pool = stack.enter_context(tc.tile_pool(name="weight", bufs=4))
+        raw_pool = stack.enter_context(tc.tile_pool(name="raw", bufs=SLABS + CHUNKS))
         x_grouped_pool = stack.enter_context(tc.tile_pool(name="x_grouped", bufs=3))
-        u_pool = stack.enter_context(tc.tile_pool(name="u", bufs=4))
+        u_pool = stack.enter_context(tc.tile_pool(name="u", bufs=PIECES + 6))
         grouped_pool = stack.enter_context(tc.tile_pool(name="grouped", bufs=4))
         u_mx_pool = stack.enter_context(tc.tile_pool(name="u_mx", bufs=4))
-        result_pool = stack.enter_context(tc.tile_pool(name="result", bufs=4))
+        result_pool = stack.enter_context(tc.tile_pool(name="result", bufs=3))
         z_pool = stack.enter_context(tc.psum_pool(name="z", bufs=3))
         flipped_pool = stack.enter_context(tc.psum_pool(name="flipped", bufs=2))
         y_pool = stack.enter_context(tc.psum_pool(name="y", bufs=3))
@@ -63,34 +70,37 @@ def tile_getspatialgatingweights_pa_t_kernel(tc, x_norm, w1_u, b1_u, w2, b2, out
         w2_codes = keep.tile([P, CELLS], U32, align_bytes=64)
         w2_scales = keep.tile([P, CELLS], U8, align_bytes=64)
 
-        def load_weight(weight):
-            rows = u_pool.tile([P, BLOCKS * CHANNELS], BF16, tag="u")
+        def load_weight(weight, pair):
+            rows = weight_pool.tile([P, 2 * CHANNELS], BF16)
             nc.sync.dma_start(
-                out=rows[:].rearrange("r (b k) -> r b k", b=BLOCKS),
-                in_=weight.rearrange("(b r) k -> r b k", r=P),
+                out=rows[:].rearrange("r (b k) -> r b k", b=2),
+                in_=weight.rearrange("(b r) k -> r b k", r=P)[:, 2 * pair : 2 * pair + 2],
             )
             return rows
 
-        def load_chunk(n, chunk):
-            raw = raw_pool.tile([P, PACK, CHUNK], BF16)
+        def load_voxels(n, first, count):
+            raw = raw_pool.tile([P, PACK, count], BF16, tag="raw%d" % count, bufs=SLABS - 1 if count == CHUNK else 2)
             channels = x_flat[n].rearrange("(u p e) v -> u p e v", u=2, p=P, e=2)
             for u in range(2):
                 nc.sync.dma_start(
                     out=raw[:, 2 * u : 2 * u + 2, :],
-                    in_=channels[u][:, :, chunk * CHUNK : (chunk + 1) * CHUNK],
+                    in_=channels[u][:, :, first : first + count],
                 )
-            return raw
+            return [raw[:, :, i * SLAB : (i + 1) * SLAB] for i in range(count // SLAB)]
 
-        def regroup_slab(raw_chunks, slab):
-            chunk, part = divmod(slab, CHUNK // SLAB)
-            x_grouped = x_grouped_pool.tile([P, SLAB * PACK], BF16, align_bytes=64)
-            source = raw_chunks[chunk][:, :, part * SLAB : (part + 1) * SLAB].rearrange(
-                "p t (r gw pw) -> p r pw gw t", gw=GRID, pw=2
-            )
+        def slab_views(raw_slab, x_grouped):
+            source = raw_slab.rearrange("p t (r gw pw) -> p r pw gw t", gw=GRID, pw=2)
             target = x_grouped[:].rearrange("p (r pw gw t) -> p r pw gw t", pw=2, gw=GRID, t=PACK)
-            nc.vector.tensor_copy(out=target[:, 0:VECTOR_ROWS], in_=source[:, 0:VECTOR_ROWS])
-            for pw in range(2):
-                nc.scalar.copy(out=target[:, VECTOR_ROWS:SLAB_ROWS, pw], in_=source[:, VECTOR_ROWS:SLAB_ROWS, pw])
+            return source, target
+
+        def regroup_slab(raw_slab, scalar_rows):
+            x_grouped = x_grouped_pool.tile([P, SLAB * PACK], BF16, align_bytes=64)
+            source, target = slab_views(raw_slab, x_grouped)
+            split = SLAB_ROWS - scalar_rows
+            nc.vector.tensor_copy(out=target[:, 0:split], in_=source[:, 0:split])
+            if scalar_rows:
+                for pw in range(2):
+                    nc.scalar.copy(out=target[:, split:SLAB_ROWS, pw], in_=source[:, split:SLAB_ROWS, pw])
             return x_grouped
 
         def quantise_slab(n, slab, x_grouped):
@@ -99,12 +109,12 @@ def tile_getspatialgatingweights_pa_t_kernel(tc, x_norm, w1_u, b1_u, w2, b2, out
                 out=x_codes[n][:, columns].bitcast(FP8X4), scales=x_scales[n][:, columns], in_=x_grouped[:]
             )
 
-        def transpose_two_blocks(source, pair):
+        def transpose_two_blocks(source):
             words = source.bitcast(F32)
             flipped = flipped_pool.tile([P, 2, 2, P], F32, tag="flipped")
             for b in range(2):
                 for u in range(2):
-                    first = ((2 * pair + b) * 2 + u) * P
+                    first = (2 * b + u) * P
                     nc.tensor.transpose(flipped[:, b, u, :], words[:, first : first + P], identity[:])
             grouped = grouped_pool.tile([P, 2 * P * PACK], BF16, align_bytes=64)
             nc.scalar.copy(
@@ -113,21 +123,18 @@ def tile_getspatialgatingweights_pa_t_kernel(tc, x_norm, w1_u, b1_u, w2, b2, out
             )
             return grouped
 
-        def quantise_weight(rows, codes, scales):
-            halves = [transpose_two_blocks(rows[:], pair) for pair in range(2)]
-            for pair in range(2):
-                columns = slice(pair * 2 * P, (pair + 1) * 2 * P)
-                nc.vector.quantize_mx(
-                    out=codes[:, columns].bitcast(FP8X4), scales=scales[:, columns], in_=halves[pair][:]
-                )
+        def quantise_weight(grouped, pair, codes, scales):
+            columns = slice(pair * 2 * P, (pair + 1) * 2 * P)
+            nc.vector.quantize_mx(
+                out=codes[:, columns].bitcast(FP8X4), scales=scales[:, columns], in_=grouped[:]
+            )
 
-        def project(piece, u, pair):
-            n, rest = divmod(piece, 2 * BLOCKS)
-            block, pd = divmod(rest, 2)
+        def project(n, chunk, piece, u_tiles):
+            block, pd = divmod(piece, 2)
             channels = slice(block * P, (block + 1) * P)
             z = z_pool.tile([P, 2, PLANE], F32)
             for i in range(2):
-                d = 2 * (2 * pair + i) + pd
+                d = 2 * (2 * chunk + i) + pd
                 plane = slice(d * PLANE, (d + 1) * PLANE)
                 nc.tensor.matmul_mx(
                     out=z[:, i, :],
@@ -138,9 +145,11 @@ def tile_getspatialgatingweights_pa_t_kernel(tc, x_norm, w1_u, b1_u, w2, b2, out
                     start=True,
                     stop=True,
                 )
+            if chunk == 0:
+                u_tiles[n * PIECES + piece] = u_pool.tile([P, 4 * CELLS], BF16, name="u")
             nc.scalar.activation(
-                out=u[:]
-                .rearrange("c (q g) -> c q g", q=4)[:, :, pair * P : (pair + 1) * P]
+                out=u_tiles[n * PIECES + piece][:]
+                .rearrange("c (q g) -> c q g", q=4)[:, :, chunk * P : (chunk + 1) * P]
                 .rearrange("c q (a gw) -> c q a gw", gw=GRID),
                 in_=z[:].rearrange("c i (gh q gw) -> c q (i gh) gw", q=4, gw=GRID),
                 func=GELU,
@@ -148,9 +157,8 @@ def tile_getspatialgatingweights_pa_t_kernel(tc, x_norm, w1_u, b1_u, w2, b2, out
                 scale=1.0,
             )
 
-        def mix(piece, ph, u_codes, u_scales, result):
-            n, rest = divmod(piece, 2 * BLOCKS)
-            block, pd = divmod(rest, 2)
+        def mix(n, piece, ph, u_codes, u_scales, result):
+            block, pd = divmod(piece, 2)
             result_view = result[:].rearrange(
                 "c (gd gh ph gw pw) -> c ph gd gh gw pw", gd=GRID, gh=GRID, ph=2, gw=GRID, pw=2
             )
@@ -184,12 +192,19 @@ def tile_getspatialgatingweights_pa_t_kernel(tc, x_norm, w1_u, b1_u, w2, b2, out
 
         b1_rows = keep.tile([P, P], BF16)
         nc.vector.memset(b1_rows[:], 0.0)
+        raw_slabs = [[], []]
         nc.sync.dma_start(out=b1_rows[0:BLOCKS, :], in_=b1_u.rearrange("(b r) -> b r", r=P))
-        w1_rows = load_weight(w1_u)
-        raw_chunks = [load_chunk(0, chunk) for chunk in range(CHUNKS)]
-        w2_rows = load_weight(w2)
+        w1_rows = [load_weight(w1_u, 0)]
+        raw_slabs[0] += load_voxels(0, 0, SLAB)
+        w1_rows.append(load_weight(w1_u, 1))
+        raw_slabs[0] += load_voxels(0, SLAB, SLAB)
+        for chunk in range(1, CHUNKS):
+            raw_slabs[0] += load_voxels(0, chunk * CHUNK, CHUNK)
+        w2_rows = [load_weight(w2, pair) for pair in range(2)]
         b2_all = keep.tile([P, CELLS], BF16)
         nc.sync.dma_start(out=b2_all[:], in_=b2.partition_broadcast(P))
+        for chunk in range(CHUNKS):
+            raw_slabs[1] += load_voxels(1, chunk * CHUNK, CHUNK)
 
         b1_rows_f32 = keep.tile([P, P], F32)
         nc.vector.tensor_copy(out=b1_rows_f32[:], in_=b1_rows[:])
@@ -197,43 +212,70 @@ def tile_getspatialgatingweights_pa_t_kernel(tc, x_norm, w1_u, b1_u, w2, b2, out
         nc.tensor.transpose(b1_flipped[:, 0, 0, :], b1_rows_f32[:], identity[:])
         b1_columns = keep.tile([P, BLOCKS], F32)
         nc.vector.tensor_copy(out=b1_columns[:], in_=b1_flipped[:, 0, 0, 0:BLOCKS])
-
-        quantise_weight(w1_rows, w1_codes, w1_scales)
-        waiting = regroup_slab(raw_chunks, 0)
-        for slab in range(1, SLABS):
-            x_grouped = regroup_slab(raw_chunks, slab)
-            quantise_slab(0, slab - 1, waiting)
-            waiting = x_grouped
-        quantise_slab(0, SLABS - 1, waiting)
-        raw_chunks = [load_chunk(1, chunk) for chunk in range(CHUNKS)]
+        w1_grouped = [transpose_two_blocks(w1_rows[0][:])]
+        x_grouped = [regroup_slab(raw_slabs[0][0], HEAD_SCALAR_ROWS)]
+        quantise_weight(w1_grouped[0], 0, w1_codes, w1_scales)
+        x_grouped.append(regroup_slab(raw_slabs[0][1], HEAD_SCALAR_ROWS))
+        w1_grouped.append(transpose_two_blocks(w1_rows[1][:]))
+        quantise_slab(0, 0, x_grouped[0])
+        quantise_slab(0, 1, x_grouped[1])
+        quantise_weight(w1_grouped[1], 1, w1_codes, w1_scales)
 
         u_tiles = {}
+        for chunk in range(1, CHUNKS):
+            x_grouped = [regroup_slab(raw_slabs[0][2 * chunk + i], 0) for i in range(2)]
+            for i in range(2):
+                quantise_slab(0, 2 * chunk + i, x_grouped[i])
+            if chunk <= CHUNKS // 2:
+                for piece in range(PIECES):
+                    project(0, chunk - 1, piece, u_tiles)
+            if chunk == 1:
+                w2_grouped = [transpose_two_blocks(w2_rows[pair][:]) for pair in range(2)]
+            if chunk == 2:
+                for pair in range(2):
+                    quantise_weight(w2_grouped[pair], pair, w2_codes, w2_scales)
+        for slab in range(EARLY_SLABS):
+            late = regroup_slab(raw_slabs[1][slab], 0)
+            quantise_slab(1, slab, late)
+        for i in range(LEAD):
+            project(0, CHUNKS // 2 + i % 2, i // 2, u_tiles)
+
+        half_chunks = CHUNKS // 2
+        project_ticks = {}
+        for n in range(BATCH):
+            for i in range(PIECES * half_chunks):
+                piece, chunk = divmod(i, half_chunks)
+                project_ticks.setdefault(n * FLIPS + i - LEAD, []).append((n, half_chunks + chunk, piece))
+        for i in range(PIECES):
+            chunk, piece = divmod(i, PIECES // 2)
+            project_ticks[FIRST_TICK + i].append((1, chunk, piece))
+            piece, chunk = divmod(i, half_chunks)
+            project_ticks[FIRST_TICK + PIECES + 2 + i * 3 // 2].append((1, chunk, PIECES // 2 + piece))
         grouped_tiles = {}
         operands = {}
         results = {}
-        for k in range(2 * PIECES + MIX_LAG):
-            if k < 2 * SLABS and k % 2 == 0:
-                x_grouped = regroup_slab(raw_chunks, k // 2)
-            if k < 2 * PIECES:
-                if k % 2 == 0:
-                    u_tiles[k // 2] = u_pool.tile([P, 4 * CELLS], BF16, tag="u", name="u")
-                for pair in (2 * (k % 2), 2 * (k % 2) + 1):
-                    project(k // 2, u_tiles[k // 2], pair)
-            if k == 1:
-                quantise_weight(w2_rows, w2_codes, w2_scales)
-            flip = k - FLIP_LAG
-            if 0 <= flip < 2 * PIECES:
-                grouped_tiles[flip] = transpose_two_blocks(u_tiles[flip // 2][:], flip % 2)
-            mixed = k - MIX_LAG
-            if 0 <= mixed < 2 * PIECES:
+        for tick in range(BATCH * FLIPS + MIX_LAG):
+            mixed = tick - MIX_LAG
+            if mixed >= 0:
                 if mixed % 2 == 0:
                     results[mixed // 2] = result_pool.tile([P, VOXELS // 2], F32, name="result")
                 u_codes, u_scales = operands[mixed]
-                mix(mixed // 2, mixed % 2, u_codes, u_scales, results[mixed // 2])
-            if 0 <= flip < 2 * PIECES:
+                n, piece = divmod(mixed // 2, PIECES)
+                mix(n, piece, mixed % 2, u_codes, u_scales, results[mixed // 2])
+            if tick % 2 == 0 and tick < BATCH * FLIPS:
+                for half in range(2):
+                    grouped_tiles[tick + half] = transpose_two_blocks(
+                        u_tiles[tick // 2][:, 2 * half * CELLS : 2 * (half + 1) * CELLS]
+                    )
+            if tick in SLAB_TICKS:
+                slab = SLAB_TICKS.index(tick) + EARLY_SLABS
+                late = regroup_slab(raw_slabs[1][slab], LATE_SCALAR_ROWS)
+            for n, chunk, piece in project_ticks.get(tick, []):
+                project(n, chunk, piece, u_tiles)
+            if tick < BATCH * FLIPS:
                 u_codes = u_mx_pool.tile([P, 2 * P], U32, align_bytes=64)
                 u_scales = u_mx_pool.tile([P, 2 * P], U8, align_bytes=64)
-                nc.vector.quantize_mx(out=u_codes[:].bitcast(FP8X4), scales=u_scales[:], in_=grouped_tiles[flip][:])
-                operands[flip] = (u_codes, u_scales)
-            if k < 2 * SLABS and k % 2 == 1:
-                quantise_slab(1, k // 2, x_grouped)
+                nc.vector.quantize_mx(out=u_codes[:].bitcast(FP8X4), scales=u_scales[:], in_=grouped_tiles[tick][:])
+                operands[tick] = (u_codes, u_scales)
+            if tick in SLAB_TICKS:
+                quantise_slab(1, slab, late)

@@ -89,8 +89,8 @@ def tile_getspatialgatingweights_pa_t_kernel(tc, x_norm, w1_u, b1_u, w2, b2, out
             return [raw[:, :, i * SLAB : (i + 1) * SLAB] for i in range(count // SLAB)]
 
         def slab_views(raw_slab, x_grouped):
-            source = raw_slab.rearrange("p t (r gw pw) -> p r pw gw t", gw=GRID, pw=2)
-            target = x_grouped[:].rearrange("p (r pw gw t) -> p r pw gw t", pw=2, gw=GRID, t=PACK)
+            source = raw_slab.rearrange("p t (r gw pw) -> p r pw t gw", gw=GRID, pw=2)
+            target = x_grouped[:].rearrange("p (r pw gw t) -> p r pw t gw", pw=2, gw=GRID, t=PACK)
             return source, target
 
         def regroup_slab(raw_slab, scalar_rows):

@@ -10,6 +10,7 @@ U8 = mybir.dt.uint8
 FP8X4 = mybir.dt.float8_e4m3fn_x4
 GELU = mybir.ActivationFunctionType.Gelu
 ADD = mybir.AluOpType.add
+MULT = mybir.AluOpType.mult
 
 P = 128
 PACK = 4
@@ -27,14 +28,10 @@ SLABS = VOXELS // SLAB
 SLAB_ROWS = SLAB // SIDE
 CHUNK = 2 * SLAB
 CHUNKS = VOXELS // CHUNK
-BANKS = CHUNKS * PIECES
 HALF = CELLS // 2
-FLIPS = 2 * PIECES
-FIRST_TICK = 2
-LEAD = 3
+HALF_CHUNKS = CHUNKS // 2
+FIRST_STEP = 2
 EARLY_SLABS = 1
-SLAB_TICKS = [2 * i for i in range(SLABS - EARLY_SLABS)]
-MIX_LAG = 2
 HEAD_SCALAR_ROWS = 12
 LATE_SCALAR_ROWS = 8
 
@@ -50,7 +47,8 @@ def tile_getspatialgatingweights_pa_t_kernel(tc, x_norm, w1_u, b1_u, w2, b2, out
         keep = stack.enter_context(tc.tile_pool(name="keep", bufs=1))
         weight_pool = stack.enter_context(tc.tile_pool(name="weight", bufs=4))
         raw_pool = stack.enter_context(tc.tile_pool(name="raw", bufs=SLABS + CHUNKS))
-        x_grouped_pool = stack.enter_context(tc.tile_pool(name="x_grouped", bufs=3))
+        x_grouped_pool = stack.enter_context(tc.tile_pool(name="x_grouped", bufs=2))
+        late_pool = stack.enter_context(tc.tile_pool(name="late", bufs=1))
         u_pool = stack.enter_context(tc.tile_pool(name="u", bufs=PIECES + 6))
         grouped_pool = stack.enter_context(tc.tile_pool(name="grouped", bufs=4))
         u_mx_pool = stack.enter_context(tc.tile_pool(name="u_mx", bufs=4))
@@ -78,26 +76,44 @@ def tile_getspatialgatingweights_pa_t_kernel(tc, x_norm, w1_u, b1_u, w2, b2, out
             )
             return rows
 
-        def load_voxels(n, first, count):
-            raw = raw_pool.tile([P, PACK, count], BF16, tag="raw%d" % count, bufs=SLABS - 1 if count == CHUNK else 2)
+        def load_planes(n, pd):
+            raw = raw_pool.tile([P, PACK, SLAB], BF16, tag="raw_slab", bufs=2)
+            channels = x_flat[n].rearrange("(u p e) (i pd v) -> u pd p e i v", u=2, p=P, e=2, pd=2, v=PLANE)
+            for u in range(2):
+                for e in range(2):
+                    nc.sync.dma_start(
+                        out=raw[:, 2 * u + e].rearrange("p (i v) -> p i v", i=2),
+                        in_=channels[u, pd, :, e, 0:2],
+                    )
+            return raw[:]
+
+        def load_chunk(n, chunk):
+            raw = raw_pool.tile([P, PACK, CHUNK], BF16, tag="raw_chunk", bufs=2 * CHUNKS - 1)
             channels = x_flat[n].rearrange("(u p e) v -> u p e v", u=2, p=P, e=2)
             for u in range(2):
                 nc.sync.dma_start(
                     out=raw[:, 2 * u : 2 * u + 2, :],
-                    in_=channels[u][:, :, first : first + count],
+                    in_=channels[u][:, :, chunk * CHUNK : (chunk + 1) * CHUNK],
                 )
-            return [raw[:, :, i * SLAB : (i + 1) * SLAB] for i in range(count // SLAB)]
+            return [raw[:, :, i * SLAB : (i + 1) * SLAB] for i in range(2)]
 
-        def slab_views(raw_slab, x_grouped):
+        def regroup_slab(raw_slab, scalar_rows, pool, engine):
+            x_grouped = pool.tile([P, SLAB * PACK], BF16, align_bytes=64, name="x_grouped")
             source = raw_slab.rearrange("p t (r gw pw) -> p r pw t gw", gw=GRID, pw=2)
             target = x_grouped[:].rearrange("p (r pw gw t) -> p r pw t gw", pw=2, gw=GRID, t=PACK)
-            return source, target
-
-        def regroup_slab(raw_slab, scalar_rows):
-            x_grouped = x_grouped_pool.tile([P, SLAB * PACK], BF16, align_bytes=64)
-            source, target = slab_views(raw_slab, x_grouped)
             split = SLAB_ROWS - scalar_rows
-            nc.vector.tensor_copy(out=target[:, 0:split], in_=source[:, 0:split])
+            if engine is nc.vector:
+                nc.vector.tensor_copy(out=target[:, 0:split], in_=source[:, 0:split])
+            else:
+                for pw in range(2):
+                    nc.gpsimd.tensor_scalar(
+                        out=target[:, 0:split, pw],
+                        in0=source[:, 0:split, pw],
+                        scalar1=1.0,
+                        scalar2=0.0,
+                        op0=MULT,
+                        op1=ADD,
+                    )
             if scalar_rows:
                 for pw in range(2):
                     nc.scalar.copy(out=target[:, split:SLAB_ROWS, pw], in_=source[:, split:SLAB_ROWS, pw])
@@ -109,7 +125,7 @@ def tile_getspatialgatingweights_pa_t_kernel(tc, x_norm, w1_u, b1_u, w2, b2, out
                 out=x_codes[n][:, columns].bitcast(FP8X4), scales=x_scales[n][:, columns], in_=x_grouped[:]
             )
 
-        def transpose_two_blocks(source):
+        def transpose_two_blocks(source, copy):
             words = source.bitcast(F32)
             flipped = flipped_pool.tile([P, 2, 2, P], F32, tag="flipped")
             for b in range(2):
@@ -117,7 +133,7 @@ def tile_getspatialgatingweights_pa_t_kernel(tc, x_norm, w1_u, b1_u, w2, b2, out
                     first = (2 * b + u) * P
                     nc.tensor.transpose(flipped[:, b, u, :], words[:, first : first + P], identity[:])
             grouped = grouped_pool.tile([P, 2 * P * PACK], BF16, align_bytes=64)
-            nc.scalar.copy(
+            copy(
                 out=grouped[:].bitcast(F32).rearrange("p (b r u) -> p b r u", b=2, r=P, u=2),
                 in_=flipped[:].rearrange("p b u r -> p b r u"),
             )
@@ -134,8 +150,8 @@ def tile_getspatialgatingweights_pa_t_kernel(tc, x_norm, w1_u, b1_u, w2, b2, out
             channels = slice(block * P, (block + 1) * P)
             z = z_pool.tile([P, 2, PLANE], F32)
             for i in range(2):
-                d = 2 * (2 * chunk + i) + pd
-                plane = slice(d * PLANE, (d + 1) * PLANE)
+                place = 2 * pd + i if n == 0 and chunk == 0 else 2 * i + pd
+                plane = slice(chunk * CHUNK + place * PLANE, chunk * CHUNK + (place + 1) * PLANE)
                 nc.tensor.matmul_mx(
                     out=z[:, i, :],
                     lhsT=w1_codes[:, channels].bitcast(FP8X4),
@@ -157,54 +173,53 @@ def tile_getspatialgatingweights_pa_t_kernel(tc, x_norm, w1_u, b1_u, w2, b2, out
                 scale=1.0,
             )
 
-        def mix(n, piece, ph, u_codes, u_scales, result):
+        def mix(n, piece, ph, half, u_codes, u_scales, result):
             block, pd = divmod(piece, 2)
             result_view = result[:].rearrange(
                 "c (gd gh ph gw pw) -> c ph gd gh gw pw", gd=GRID, gh=GRID, ph=2, gw=GRID, pw=2
             )
-            for half in range(2):
-                cells = slice(half * HALF, (half + 1) * HALF)
-                y = y_pool.tile([P, 2, HALF], F32)
-                for pw in range(2):
-                    nc.tensor.matmul_mx(
-                        out=y[:, pw, :],
-                        lhsT=u_codes[:, pw * P : (pw + 1) * P].bitcast(FP8X4),
-                        lhsT_scale=u_scales[:, pw * P : (pw + 1) * P],
-                        rhs=w2_codes[:, cells].bitcast(FP8X4),
-                        rhs_scale=w2_scales[:, cells],
-                        start=True,
-                        stop=True,
-                    )
-                nc.vector.tensor_tensor(
-                    out=result_view[:, ph, half * 4 : (half + 1) * 4],
-                    in0=y[:].rearrange("c pw (gd gh gw) -> c gd gh gw pw", gd=4, gh=GRID),
-                    in1=b2_all[:, cells]
-                    .rearrange("c (gd gh gw) -> c gd gh gw", gd=4, gh=GRID)
-                    .unsqueeze(4)
-                    .to_broadcast([P, 4, GRID, GRID, 2]),
-                    op=ADD,
+            cells = slice(half * HALF, (half + 1) * HALF)
+            y = y_pool.tile([P, 2, HALF], F32)
+            for pw in range(2):
+                nc.tensor.matmul_mx(
+                    out=y[:, pw, :],
+                    lhsT=u_codes[:, pw * P : (pw + 1) * P].bitcast(FP8X4),
+                    lhsT_scale=u_scales[:, pw * P : (pw + 1) * P],
+                    rhs=w2_codes[:, cells].bitcast(FP8X4),
+                    rhs_scale=w2_scales[:, cells],
+                    start=True,
+                    stop=True,
                 )
-                if ph == 1:
-                    nc.sync.dma_start(
-                        out=out_planes[n, block * P : (block + 1) * P, pd, half * 4 : (half + 1) * 4],
-                        in_=result[:].rearrange("c (gd v) -> c gd v", gd=GRID)[:, half * 4 : (half + 1) * 4],
-                    )
+            nc.vector.tensor_tensor(
+                out=result_view[:, ph, half * 4 : (half + 1) * 4],
+                in0=y[:].rearrange("c pw (gd gh gw) -> c gd gh gw pw", gd=4, gh=GRID),
+                in1=b2_all[:, cells]
+                .rearrange("c (gd gh gw) -> c gd gh gw", gd=4, gh=GRID)
+                .unsqueeze(4)
+                .to_broadcast([P, 4, GRID, GRID, 2]),
+                op=ADD,
+            )
+            if ph == 1:
+                nc.sync.dma_start(
+                    out=out_planes[n, block * P : (block + 1) * P, pd, half * 4 : (half + 1) * 4],
+                    in_=result[:].rearrange("c (gd v) -> c gd v", gd=GRID)[:, half * 4 : (half + 1) * 4],
+                )
 
         b1_rows = keep.tile([P, P], BF16)
         nc.vector.memset(b1_rows[:], 0.0)
         raw_slabs = [[], []]
         nc.sync.dma_start(out=b1_rows[0:BLOCKS, :], in_=b1_u.rearrange("(b r) -> b r", r=P))
         w1_rows = [load_weight(w1_u, 0)]
-        raw_slabs[0] += load_voxels(0, 0, SLAB)
+        raw_slabs[0].append(load_planes(0, 0))
         w1_rows.append(load_weight(w1_u, 1))
-        raw_slabs[0] += load_voxels(0, SLAB, SLAB)
+        raw_slabs[0].append(load_planes(0, 1))
         for chunk in range(1, CHUNKS):
-            raw_slabs[0] += load_voxels(0, chunk * CHUNK, CHUNK)
+            raw_slabs[0] += load_chunk(0, chunk)
         w2_rows = [load_weight(w2, pair) for pair in range(2)]
         b2_all = keep.tile([P, CELLS], BF16)
         nc.sync.dma_start(out=b2_all[:], in_=b2.partition_broadcast(P))
         for chunk in range(CHUNKS):
-            raw_slabs[1] += load_voxels(1, chunk * CHUNK, CHUNK)
+            raw_slabs[1] += load_chunk(1, chunk)
 
         b1_rows_f32 = keep.tile([P, P], F32)
         nc.vector.tensor_copy(out=b1_rows_f32[:], in_=b1_rows[:])
@@ -212,70 +227,87 @@ def tile_getspatialgatingweights_pa_t_kernel(tc, x_norm, w1_u, b1_u, w2, b2, out
         nc.tensor.transpose(b1_flipped[:, 0, 0, :], b1_rows_f32[:], identity[:])
         b1_columns = keep.tile([P, BLOCKS], F32)
         nc.vector.tensor_copy(out=b1_columns[:], in_=b1_flipped[:, 0, 0, 0:BLOCKS])
-        w1_grouped = [transpose_two_blocks(w1_rows[0][:])]
-        x_grouped = [regroup_slab(raw_slabs[0][0], HEAD_SCALAR_ROWS)]
-        quantise_weight(w1_grouped[0], 0, w1_codes, w1_scales)
-        x_grouped.append(regroup_slab(raw_slabs[0][1], HEAD_SCALAR_ROWS))
-        w1_grouped.append(transpose_two_blocks(w1_rows[1][:]))
-        quantise_slab(0, 0, x_grouped[0])
-        quantise_slab(0, 1, x_grouped[1])
-        quantise_weight(w1_grouped[1], 1, w1_codes, w1_scales)
-
         u_tiles = {}
+        w1_grouped = transpose_two_blocks(w1_rows[0][:], nc.scalar.copy)
+        x_grouped = regroup_slab(raw_slabs[0][0], HEAD_SCALAR_ROWS, x_grouped_pool, nc.vector)
+        quantise_weight(w1_grouped, 0, w1_codes, w1_scales)
+        w1_grouped = transpose_two_blocks(w1_rows[1][:], nc.scalar.copy)
+        quantise_slab(0, 0, x_grouped)
+        for block in range(2):
+            project(0, 0, 2 * block, u_tiles)
+        quantise_weight(w1_grouped, 1, w1_codes, w1_scales)
+        for block in range(2, BLOCKS):
+            project(0, 0, 2 * block, u_tiles)
+        x_grouped = regroup_slab(raw_slabs[0][1], 0, x_grouped_pool, nc.vector)
+        quantise_slab(0, 1, x_grouped)
+
         for chunk in range(1, CHUNKS):
-            x_grouped = [regroup_slab(raw_slabs[0][2 * chunk + i], 0) for i in range(2)]
+            x_grouped = [regroup_slab(raw_slabs[0][2 * chunk + i], 0, x_grouped_pool, nc.vector) for i in range(2)]
             for i in range(2):
                 quantise_slab(0, 2 * chunk + i, x_grouped[i])
-            if chunk <= CHUNKS // 2:
-                for piece in range(PIECES):
-                    project(0, chunk - 1, piece, u_tiles)
             if chunk == 1:
-                w2_grouped = [transpose_two_blocks(w2_rows[pair][:]) for pair in range(2)]
+                for block in range(BLOCKS):
+                    project(0, 0, 2 * block + 1, u_tiles)
             if chunk == 2:
-                for pair in range(2):
-                    quantise_weight(w2_grouped[pair], pair, w2_codes, w2_scales)
+                for piece in range(PIECES):
+                    project(0, 1, piece, u_tiles)
+        w2_grouped = [transpose_two_blocks(w2_rows[pair][:], nc.vector.tensor_copy) for pair in range(2)]
+        for pair in range(2):
+            quantise_weight(w2_grouped[pair], pair, w2_codes, w2_scales)
         for slab in range(EARLY_SLABS):
-            late = regroup_slab(raw_slabs[1][slab], 0)
-            quantise_slab(1, slab, late)
-        for i in range(LEAD):
-            project(0, CHUNKS // 2 + i % 2, i // 2, u_tiles)
-
-        half_chunks = CHUNKS // 2
-        project_ticks = {}
-        for n in range(BATCH):
-            for i in range(PIECES * half_chunks):
-                piece, chunk = divmod(i, half_chunks)
-                project_ticks.setdefault(n * FLIPS + i - LEAD, []).append((n, half_chunks + chunk, piece))
-        for i in range(PIECES):
-            chunk, piece = divmod(i, PIECES // 2)
-            project_ticks[FIRST_TICK + i].append((1, chunk, piece))
-            piece, chunk = divmod(i, half_chunks)
-            project_ticks[FIRST_TICK + PIECES + 2 + i * 3 // 2].append((1, chunk, PIECES // 2 + piece))
+            x_grouped = regroup_slab(raw_slabs[1][slab], 0, x_grouped_pool, nc.vector)
+            quantise_slab(1, slab, x_grouped)
+        late = {EARLY_SLABS: regroup_slab(raw_slabs[1][EARLY_SLABS], 0, late_pool, nc.vector)}
         grouped_tiles = {}
+
+        def flip(step):
+            for ph in range(2):
+                grouped_tiles[step, ph] = transpose_two_blocks(
+                    u_tiles[step][:, 2 * ph * CELLS : 2 * (ph + 1) * CELLS], nc.scalar.copy
+                )
+
+        for chunk, piece in ((2, 0), (3, 0), (2, 1)):
+            project(0, chunk, piece, u_tiles)
+        flip(0)
+        project(0, 3, 1, u_tiles)
+
+        project_steps = {}
+        for step in range(2, BATCH * PIECES):
+            n, piece = divmod(step, PIECES)
+            for chunk in range(HALF_CHUNKS, CHUNKS):
+                project_steps.setdefault(step - 2, []).append((n, chunk, piece))
+        for i in range(PIECES * HALF_CHUNKS):
+            piece, chunk = divmod(i, HALF_CHUNKS)
+            project_steps[FIRST_STEP + i * 3 // 4].append((1, chunk, piece))
         operands = {}
-        results = {}
-        for tick in range(BATCH * FLIPS + MIX_LAG):
-            mixed = tick - MIX_LAG
-            if mixed >= 0:
-                if mixed % 2 == 0:
-                    results[mixed // 2] = result_pool.tile([P, VOXELS // 2], F32, name="result")
-                u_codes, u_scales = operands[mixed]
-                n, piece = divmod(mixed // 2, PIECES)
-                mix(n, piece, mixed % 2, u_codes, u_scales, results[mixed // 2])
-            if tick % 2 == 0 and tick < BATCH * FLIPS:
+        for step in range(BATCH * PIECES + 1):
+            projects = project_steps.get(step, [])
+            n, piece = divmod(step - 1, PIECES)
+            if step >= 1:
+                result = result_pool.tile([P, VOXELS // 2], F32, name="result")
                 for half in range(2):
-                    grouped_tiles[tick + half] = transpose_two_blocks(
-                        u_tiles[tick // 2][:, 2 * half * CELLS : 2 * (half + 1) * CELLS]
+                    mix(n, piece, 0, half, *operands[step - 1, 0], result)
+            if len(projects) > 2:
+                project(*projects.pop(2), u_tiles)
+            if step + 1 < BATCH * PIECES:
+                flip(step + 1)
+            if step < BATCH * PIECES:
+                for ph in range(2):
+                    u_codes = u_mx_pool.tile([P, 2 * P], U32, align_bytes=64)
+                    u_scales = u_mx_pool.tile([P, 2 * P], U8, align_bytes=64)
+                    nc.vector.quantize_mx(
+                        out=u_codes[:].bitcast(FP8X4), scales=u_scales[:], in_=grouped_tiles[step, ph][:]
                     )
-            if tick in SLAB_TICKS:
-                slab = SLAB_TICKS.index(tick) + EARLY_SLABS
-                late = regroup_slab(raw_slabs[1][slab], LATE_SCALAR_ROWS)
-            for n, chunk, piece in project_ticks.get(tick, []):
-                project(n, chunk, piece, u_tiles)
-            if tick < BATCH * FLIPS:
-                u_codes = u_mx_pool.tile([P, 2 * P], U32, align_bytes=64)
-                u_scales = u_mx_pool.tile([P, 2 * P], U8, align_bytes=64)
-                nc.vector.quantize_mx(out=u_codes[:].bitcast(FP8X4), scales=u_scales[:], in_=grouped_tiles[tick][:])
-                operands[tick] = (u_codes, u_scales)
-            if tick in SLAB_TICKS:
-                quantise_slab(1, slab, late)
+                    operands[step, ph] = (u_codes, u_scales)
+            slab = step + EARLY_SLABS
+            if slab < SLABS:
+                quantise_slab(1, slab, late[slab])
+            if slab + 1 < SLABS:
+                late[slab + 1] = regroup_slab(raw_slabs[1][slab + 1], LATE_SCALAR_ROWS, late_pool, nc.gpsimd)
+            for half in range(2):
+                if projects:
+                    project(*projects.pop(0), u_tiles)
+                if step >= 1:
+                    mix(n, piece, 1, half, *operands[step - 1, 1], result)
+            for bank in projects:
+                project(*bank, u_tiles)

@@ -190,20 +190,25 @@ def tile_getspatialgatingweights_pa_t_kernel(tc, x_norm, w1_u, b1_u, w2, b2, out
                     start=True,
                     stop=True,
                 )
-            nc.vector.tensor_tensor(
-                out=result_view[:, ph, half * 4 : (half + 1) * 4],
-                in0=y[:].rearrange("c pw (gd gh gw) -> c gd gh gw pw", gd=4, gh=GRID),
-                in1=b2_all[:, cells]
-                .rearrange("c (gd gh gw) -> c gd gh gw", gd=4, gh=GRID)
-                .unsqueeze(4)
-                .to_broadcast([P, 4, GRID, GRID, 2]),
-                op=ADD,
-            )
-            if ph == 1:
-                nc.sync.dma_start(
-                    out=out_planes[n, block * P : (block + 1) * P, pd, half * 4 : (half + 1) * 4],
-                    in_=result[:].rearrange("c (gd v) -> c gd v", gd=GRID)[:, half * 4 : (half + 1) * 4],
+            parts = 2 if (n, piece, ph, half) == (BATCH - 1, PIECES - 1, 1, 1) else 1
+            for part in range(parts):
+                gd = slice(4 * half + part * 4 // parts, 4 * half + (part + 1) * 4 // parts)
+                nc.vector.tensor_tensor(
+                    out=result_view[:, ph, gd],
+                    in0=y[:].rearrange("c pw (gd gh gw) -> c gd gh gw pw", gd=4, gh=GRID)[
+                        :, part * 4 // parts : (part + 1) * 4 // parts
+                    ],
+                    in1=b2_all[:]
+                    .rearrange("c (gd gh gw) -> c gd gh gw", gd=GRID, gh=GRID)[:, gd]
+                    .unsqueeze(4)
+                    .to_broadcast([P, 4 // parts, GRID, GRID, 2]),
+                    op=ADD,
                 )
+                if ph == 1:
+                    nc.sync.dma_start(
+                        out=out_planes[n, block * P : (block + 1) * P, pd, gd],
+                        in_=result[:].rearrange("c (gd v) -> c gd v", gd=GRID)[:, gd],
+                    )
 
         b1_rows = keep.tile([P, P], BF16)
         nc.vector.memset(b1_rows[:], 0.0)
@@ -285,8 +290,8 @@ def tile_getspatialgatingweights_pa_t_kernel(tc, x_norm, w1_u, b1_u, w2, b2, out
             n, piece = divmod(step - 1, PIECES)
             if step >= 1:
                 result = result_pool.tile([P, VOXELS // 2], F32, name="result")
-                for half in range(2):
-                    mix(n, piece, 0, half, *operands[step - 1, 0], result)
+                for ph in range(2):
+                    mix(n, piece, ph, 0, *operands[step - 1, ph], result)
             if len(projects) > 2:
                 project(*projects.pop(2), u_tiles)
             if step + 1 < BATCH * PIECES:
@@ -304,10 +309,10 @@ def tile_getspatialgatingweights_pa_t_kernel(tc, x_norm, w1_u, b1_u, w2, b2, out
                 quantise_slab(1, slab, late[slab])
             if slab + 1 < SLABS:
                 late[slab + 1] = regroup_slab(raw_slabs[1][slab + 1], LATE_SCALAR_ROWS, late_pool, nc.gpsimd)
-            for half in range(2):
+            for ph in range(2):
                 if projects:
                     project(*projects.pop(0), u_tiles)
                 if step >= 1:
-                    mix(n, piece, 1, half, *operands[step - 1, 1], result)
+                    mix(n, piece, ph, 1, *operands[step - 1, ph], result)
             for bank in projects:
                 project(*bank, u_tiles)

@@ -33,6 +33,7 @@ HALF_CHUNKS = CHUNKS // 2
 FIRST_STEP = 2
 EARLY_SLABS = 1
 HEAD_SCALAR_ROWS = 12
+SECOND_SCALAR_ROWS = 8
 LATE_SCALAR_ROWS = 8
 
 FLOPS = 2 * 2 * BATCH * CHANNELS * CHANNELS * VOXELS
@@ -50,8 +51,8 @@ def tile_getspatialgatingweights_pa_t_kernel(tc, x_norm, w1_u, b1_u, w2, b2, out
         x_grouped_pool = stack.enter_context(tc.tile_pool(name="x_grouped", bufs=2))
         late_pool = stack.enter_context(tc.tile_pool(name="late", bufs=1))
         u_pool = stack.enter_context(tc.tile_pool(name="u", bufs=PIECES + 6))
-        grouped_pool = stack.enter_context(tc.tile_pool(name="grouped", bufs=4))
-        u_mx_pool = stack.enter_context(tc.tile_pool(name="u_mx", bufs=4))
+        grouped_pool = stack.enter_context(tc.tile_pool(name="grouped", bufs=2))
+        u_mx_pool = stack.enter_context(tc.tile_pool(name="u_mx", bufs=2))
         result_pool = stack.enter_context(tc.tile_pool(name="result", bufs=3))
         z_pool = stack.enter_context(tc.psum_pool(name="z", bufs=3))
         flipped_pool = stack.enter_context(tc.psum_pool(name="flipped", bufs=2))
@@ -97,27 +98,37 @@ def tile_getspatialgatingweights_pa_t_kernel(tc, x_norm, w1_u, b1_u, w2, b2, out
                 )
             return [raw[:, :, i * SLAB : (i + 1) * SLAB] for i in range(2)]
 
-        def regroup_slab(raw_slab, scalar_rows, pool, engine):
+        def regroup_slab(raw_slab, scalar_rows, pool, engine, vector_rows=0):
             x_grouped = pool.tile([P, SLAB * PACK], BF16, align_bytes=64, name="x_grouped")
             source = raw_slab.rearrange("p t (r gw pw) -> p r pw t gw", gw=GRID, pw=2)
             target = x_grouped[:].rearrange("p (r pw gw t) -> p r pw t gw", pw=2, gw=GRID, t=PACK)
             split = SLAB_ROWS - scalar_rows
+            if engine is nc.gpsimd and vector_rows:
+                rows = slice(split - vector_rows, split)
+                nc.vector.tensor_copy(out=target[:, rows], in_=source[:, rows])
             if engine is nc.vector:
                 nc.vector.tensor_copy(out=target[:, 0:split], in_=source[:, 0:split])
             else:
                 for pw in range(2):
                     nc.gpsimd.tensor_scalar(
-                        out=target[:, 0:split, pw],
-                        in0=source[:, 0:split, pw],
+                        out=target[:, 0 : split - vector_rows, pw],
+                        in0=source[:, 0 : split - vector_rows, pw],
                         scalar1=1.0,
                         scalar2=0.0,
                         op0=MULT,
                         op1=ADD,
                     )
-            if scalar_rows:
+            if scalar_rows and engine is nc.vector:
                 for pw in range(2):
                     nc.scalar.copy(out=target[:, split:SLAB_ROWS, pw], in_=source[:, split:SLAB_ROWS, pw])
             return x_grouped
+
+        def regroup_rest(raw_slab, scalar_rows, x_grouped):
+            source = raw_slab.rearrange("p t (r gw pw) -> p r pw t gw", gw=GRID, pw=2)
+            target = x_grouped[:].rearrange("p (r pw gw t) -> p r pw t gw", pw=2, gw=GRID, t=PACK)
+            split = SLAB_ROWS - scalar_rows
+            for pw in range(2):
+                nc.scalar.copy(out=target[:, split:SLAB_ROWS, pw], in_=source[:, split:SLAB_ROWS, pw])
 
         def quantise_slab(n, slab, x_grouped):
             columns = slice(slab * SLAB, (slab + 1) * SLAB)
@@ -125,24 +136,26 @@ def tile_getspatialgatingweights_pa_t_kernel(tc, x_norm, w1_u, b1_u, w2, b2, out
                 out=x_codes[n][:, columns].bitcast(FP8X4), scales=x_scales[n][:, columns], in_=x_grouped[:]
             )
 
-        def transpose_two_blocks(source, copy):
+        def transpose_two_blocks(source, copy, target=None):
             words = source.bitcast(F32)
             flipped = flipped_pool.tile([P, 2, 2, P], F32, tag="flipped")
             for b in range(2):
                 for u in range(2):
                     first = (2 * b + u) * P
                     nc.tensor.transpose(flipped[:, b, u, :], words[:, first : first + P], identity[:])
-            grouped = grouped_pool.tile([P, 2 * P * PACK], BF16, align_bytes=64)
+            if target is None:
+                weight = grouped_pool.tile([P, 2 * P * PACK], BF16, align_bytes=64)
+                target = weight[:]
             copy(
-                out=grouped[:].bitcast(F32).rearrange("p (b r u) -> p b r u", b=2, r=P, u=2),
+                out=target.bitcast(F32).rearrange("p (b r u) -> p b r u", b=2, r=P, u=2),
                 in_=flipped[:].rearrange("p b u r -> p b r u"),
             )
-            return grouped
+            return target
 
         def quantise_weight(grouped, pair, codes, scales):
             columns = slice(pair * 2 * P, (pair + 1) * 2 * P)
             nc.vector.quantize_mx(
-                out=codes[:, columns].bitcast(FP8X4), scales=scales[:, columns], in_=grouped[:]
+                out=codes[:, columns].bitcast(FP8X4), scales=scales[:, columns], in_=grouped
             )
 
         def project(n, chunk, piece, u_tiles):
@@ -238,12 +251,10 @@ def tile_getspatialgatingweights_pa_t_kernel(tc, x_norm, w1_u, b1_u, w2, b2, out
         quantise_weight(w1_grouped, 0, w1_codes, w1_scales)
         w1_grouped = transpose_two_blocks(w1_rows[1][:], nc.scalar.copy)
         quantise_slab(0, 0, x_grouped)
-        for block in range(2):
-            project(0, 0, 2 * block, u_tiles)
+        x_grouped = regroup_slab(raw_slabs[0][1], SECOND_SCALAR_ROWS, x_grouped_pool, nc.vector)
         quantise_weight(w1_grouped, 1, w1_codes, w1_scales)
-        for block in range(2, BLOCKS):
+        for block in range(BLOCKS):
             project(0, 0, 2 * block, u_tiles)
-        x_grouped = regroup_slab(raw_slabs[0][1], 0, x_grouped_pool, nc.vector)
         quantise_slab(0, 1, x_grouped)
 
         for chunk in range(1, CHUNKS):
@@ -256,9 +267,6 @@ def tile_getspatialgatingweights_pa_t_kernel(tc, x_norm, w1_u, b1_u, w2, b2, out
             if chunk == 2:
                 for piece in range(PIECES):
                     project(0, 1, piece, u_tiles)
-        w2_grouped = [transpose_two_blocks(w2_rows[pair][:], nc.vector.tensor_copy) for pair in range(2)]
-        for pair in range(2):
-            quantise_weight(w2_grouped[pair], pair, w2_codes, w2_scales)
         for slab in range(EARLY_SLABS):
             x_grouped = regroup_slab(raw_slabs[1][slab], 0, x_grouped_pool, nc.vector)
             quantise_slab(1, slab, x_grouped)
@@ -266,21 +274,27 @@ def tile_getspatialgatingweights_pa_t_kernel(tc, x_norm, w1_u, b1_u, w2, b2, out
         grouped_tiles = {}
 
         def flip(step):
+            piece = grouped_pool.tile([P, CELLS * PACK], BF16, align_bytes=64)
             for ph in range(2):
-                grouped_tiles[step, ph] = transpose_two_blocks(
-                    u_tiles[step][:, 2 * ph * CELLS : 2 * (ph + 1) * CELLS], nc.scalar.copy
-                )
+                part = slice(2 * ph * CELLS, 2 * (ph + 1) * CELLS)
+                transpose_two_blocks(u_tiles[step][:, part], nc.scalar.copy, piece[:, part])
+            grouped_tiles[step] = piece
 
-        for chunk, piece in ((2, 0), (3, 0), (2, 1)):
-            project(0, chunk, piece, u_tiles)
+        project(0, 2, 0, u_tiles)
+        w2_grouped = [transpose_two_blocks(w2_rows[pair][:], nc.scalar.copy) for pair in range(2)]
+        project(0, 3, 0, u_tiles)
+        project(0, 2, 1, u_tiles)
         flip(0)
+        for pair in range(2):
+            quantise_weight(w2_grouped[pair], pair, w2_codes, w2_scales)
         project(0, 3, 1, u_tiles)
 
         project_steps = {}
         for step in range(2, BATCH * PIECES):
             n, piece = divmod(step, PIECES)
             for chunk in range(HALF_CHUNKS, CHUNKS):
-                project_steps.setdefault(step - 2, []).append((n, chunk, piece))
+                if n or chunk > HALF_CHUNKS or piece >= 2:
+                    project_steps.setdefault(step - 2, []).append((n, chunk, piece))
         for i in range(PIECES * HALF_CHUNKS):
             piece, chunk = divmod(i, HALF_CHUNKS)
             project_steps[FIRST_STEP + i * 3 // 4].append((1, chunk, piece))
@@ -290,29 +304,35 @@ def tile_getspatialgatingweights_pa_t_kernel(tc, x_norm, w1_u, b1_u, w2, b2, out
             n, piece = divmod(step - 1, PIECES)
             if step >= 1:
                 result = result_pool.tile([P, VOXELS // 2], F32, name="result")
-                for ph in range(2):
-                    mix(n, piece, ph, 0, *operands[step - 1, ph], result)
+            if step >= 1:
+                mix(n, piece, 0, 0, *operands[step - 1, 0], result)
+            if step >= 1:
+                mix(n, piece, 1, 0, *operands[step - 1, 1], result)
             if len(projects) > 2:
                 project(*projects.pop(2), u_tiles)
-            if step + 1 < BATCH * PIECES:
-                flip(step + 1)
             if step < BATCH * PIECES:
+                u_codes = u_mx_pool.tile([P, CELLS], U32, align_bytes=64)
+                u_scales = u_mx_pool.tile([P, CELLS], U8, align_bytes=64)
+                nc.vector.quantize_mx(out=u_codes[:].bitcast(FP8X4), scales=u_scales[:], in_=grouped_tiles[step][:])
                 for ph in range(2):
-                    u_codes = u_mx_pool.tile([P, 2 * P], U32, align_bytes=64)
-                    u_scales = u_mx_pool.tile([P, 2 * P], U8, align_bytes=64)
-                    nc.vector.quantize_mx(
-                        out=u_codes[:].bitcast(FP8X4), scales=u_scales[:], in_=grouped_tiles[step, ph][:]
-                    )
-                    operands[step, ph] = (u_codes, u_scales)
+                    part = slice(ph * 2 * P, (ph + 1) * 2 * P)
+                    operands[step, ph] = (u_codes[:, part], u_scales[:, part])
             slab = step + EARLY_SLABS
             if slab < SLABS:
                 quantise_slab(1, slab, late[slab])
             if slab + 1 < SLABS:
-                late[slab + 1] = regroup_slab(raw_slabs[1][slab + 1], LATE_SCALAR_ROWS, late_pool, nc.gpsimd)
-            for ph in range(2):
-                if projects:
-                    project(*projects.pop(0), u_tiles)
-                if step >= 1:
-                    mix(n, piece, ph, 1, *operands[step - 1, ph], result)
+                late[slab + 1] = regroup_slab(raw_slabs[1][slab + 1], LATE_SCALAR_ROWS, late_pool, nc.gpsimd, 12 if step == 0 else 0)
+            if step >= 1:
+                mix(n, piece, 0, 1, *operands[step - 1, 0], result)
+            if projects:
+                project(*projects.pop(0), u_tiles)
+            if step + 1 < BATCH * PIECES:
+                flip(step + 1)
+            if step >= 1:
+                mix(n, piece, 1, 1, *operands[step - 1, 1], result)
+            if projects:
+                project(*projects.pop(0), u_tiles)
             for bank in projects:
                 project(*bank, u_tiles)
+            if slab + 1 < SLABS:
+                regroup_rest(raw_slabs[1][slab + 1], LATE_SCALAR_ROWS, late[slab + 1])

from contextlib import ExitStack

import concourse.mybir as mybir
from concourse.masks import make_identity

F32 = mybir.dt.float32
BF16 = mybir.dt.bfloat16
U32 = mybir.dt.uint32
U8 = mybir.dt.uint8
FP8X4 = mybir.dt.float8_e4m3fn_x4
GELU = mybir.ActivationFunctionType.Gelu
ADD = mybir.AluOpType.add
MULT = mybir.AluOpType.mult

P = 128
PACK = 4
BATCH = 2
CHANNELS = 512
SIDE = 16
VOXELS = SIDE * SIDE * SIDE
CELLS = 512
GRID = 8
PLANE = SIDE * SIDE
BLOCKS = CHANNELS // P
PIECES = BLOCKS * 2
SLAB = 2 * PLANE
SLABS = VOXELS // SLAB
SLAB_ROWS = SLAB // SIDE
CHUNK = 2 * SLAB
CHUNKS = VOXELS // CHUNK
HALF = CELLS // 2
HALF_CHUNKS = CHUNKS // 2
FIRST_STEP = 2
EARLY_SLABS = 1
HEAD_SCALAR_ROWS = 12
SECOND_SCALAR_ROWS = 8
LATE_SCALAR_ROWS = 8

FLOPS = 2 * 2 * BATCH * CHANNELS * CHANNELS * VOXELS


def tile_getspatialgatingweights_pa_t_kernel(tc, x_norm, w1_u, b1_u, w2, b2, out):
    nc = tc.nc
    x_flat = x_norm.rearrange("n c d h w -> n c (d h w)")
    out_planes = out.rearrange("n c (gd pd) h w -> n c pd gd (h w)", pd=2)

    with ExitStack() as stack:
        keep = stack.enter_context(tc.tile_pool(name="keep", bufs=1))
        weight_pool = stack.enter_context(tc.tile_pool(name="weight", bufs=4))
        raw_pool = stack.enter_context(tc.tile_pool(name="raw", bufs=SLABS + CHUNKS))
        x_grouped_pool = stack.enter_context(tc.tile_pool(name="x_grouped", bufs=2))
        late_pool = stack.enter_context(tc.tile_pool(name="late", bufs=1))
        u_pool = stack.enter_context(tc.tile_pool(name="u", bufs=PIECES + 6))
        grouped_pool = stack.enter_context(tc.tile_pool(name="grouped", bufs=2))
        u_mx_pool = stack.enter_context(tc.tile_pool(name="u_mx", bufs=2))
        result_pool = stack.enter_context(tc.tile_pool(name="result", bufs=3))
        z_pool = stack.enter_context(tc.psum_pool(name="z", bufs=3))
        flipped_pool = stack.enter_context(tc.psum_pool(name="flipped", bufs=2))
        y_pool = stack.enter_context(tc.psum_pool(name="y", bufs=3))
        stack.enter_context(tc.manual_schedule())

        identity = keep.tile([P, P], F32)
        make_identity(nc, identity[:])

        x_codes = [keep.tile([P, VOXELS], U32, align_bytes=64, name="x_codes%d" % n) for n in range(BATCH)]
        x_scales = [keep.tile([P, VOXELS], U8, align_bytes=64, name="x_scales%d" % n) for n in range(BATCH)]
        w1_codes = keep.tile([P, CHANNELS], U32, align_bytes=64)
        w1_scales = keep.tile([P, CHANNELS], U8, align_bytes=64)
        w2_codes = keep.tile([P, CELLS], U32, align_bytes=64)
        w2_scales = keep.tile([P, CELLS], U8, align_bytes=64)

        def load_weight(weight, pair):
            rows = weight_pool.tile([P, 2 * CHANNELS], BF16)
            nc.sync.dma_start(
                out=rows[:].rearrange("r (b k) -> r b k", b=2),
                in_=weight.rearrange("(b r) k -> r b k", r=P)[:, 2 * pair : 2 * pair + 2],
            )
            return rows

        def load_planes(n, pd):
            raw = raw_pool.tile([P, PACK, SLAB], BF16, tag="raw_slab", bufs=2)
            channels = x_flat[n].rearrange("(u p e) (i pd v) -> u pd p e i v", u=2, p=P, e=2, pd=2, v=PLANE)
            for u in range(2):
                for e in range(2):
                    nc.sync.dma_start(
                        out=raw[:, 2 * u + e].rearrange("p (i v) -> p i v", i=2),
                        in_=channels[u, pd, :, e, 0:2],
                    )
            return raw[:]

        def load_chunk(n, chunk):
            raw = raw_pool.tile([P, PACK, CHUNK], BF16, tag="raw_chunk", bufs=2 * CHUNKS - 1)
            channels = x_flat[n].rearrange("(u p e) v -> u p e v", u=2, p=P, e=2)
            for u in range(2):
                nc.sync.dma_start(
                    out=raw[:, 2 * u : 2 * u + 2, :],
                    in_=channels[u][:, :, chunk * CHUNK : (chunk + 1) * CHUNK],
                )
            return [raw[:, :, i * SLAB : (i + 1) * SLAB] for i in range(2)]

        def regroup_slab(raw_slab, scalar_rows, pool, engine, vector_rows=0):
            x_grouped = pool.tile([P, SLAB * PACK], BF16, align_bytes=64, name="x_grouped")
            source = raw_slab.rearrange("p t (r gw pw) -> p r pw t gw", gw=GRID, pw=2)
            target = x_grouped[:].rearrange("p (r pw gw t) -> p r pw t gw", pw=2, gw=GRID, t=PACK)
            split = SLAB_ROWS - scalar_rows
            if engine is nc.gpsimd and vector_rows:
                rows = slice(split - vector_rows, split)
                nc.vector.tensor_copy(out=target[:, rows], in_=source[:, rows])
            if engine is nc.vector:
                nc.vector.tensor_copy(out=target[:, 0:split], in_=source[:, 0:split])
            else:
                for pw in range(2):
                    nc.gpsimd.tensor_scalar(
                        out=target[:, 0 : split - vector_rows, pw],
                        in0=source[:, 0 : split - vector_rows, pw],
                        scalar1=1.0,
                        scalar2=0.0,
                        op0=MULT,
                        op1=ADD,
                    )
            if scalar_rows and engine is nc.vector:
                for pw in range(2):
                    nc.scalar.copy(out=target[:, split:SLAB_ROWS, pw], in_=source[:, split:SLAB_ROWS, pw])
            return x_grouped

        def regroup_rest(raw_slab, scalar_rows, x_grouped):
            source = raw_slab.rearrange("p t (r gw pw) -> p r pw t gw", gw=GRID, pw=2)
            target = x_grouped[:].rearrange("p (r pw gw t) -> p r pw t gw", pw=2, gw=GRID, t=PACK)
            split = SLAB_ROWS - scalar_rows
            for pw in range(2):
                nc.scalar.copy(out=target[:, split:SLAB_ROWS, pw], in_=source[:, split:SLAB_ROWS, pw])

        def quantise_slab(n, slab, x_grouped):
            columns = slice(slab * SLAB, (slab + 1) * SLAB)
            nc.vector.quantize_mx(
                out=x_codes[n][:, columns].bitcast(FP8X4), scales=x_scales[n][:, columns], in_=x_grouped[:]
            )

        def transpose_two_blocks(source, copy, target=None):
            words = source.bitcast(F32)
            flipped = flipped_pool.tile([P, 2, 2, P], F32, tag="flipped")
            for b in range(2):
                for u in range(2):
                    first = (2 * b + u) * P
                    nc.tensor.transpose(flipped[:, b, u, :], words[:, first : first + P], identity[:])
            if target is None:
                weight = grouped_pool.tile([P, 2 * P * PACK], BF16, align_bytes=64)
                target = weight[:]
            copy(
                out=target.bitcast(F32).rearrange("p (b r u) -> p b r u", b=2, r=P, u=2),
                in_=flipped[:].rearrange("p b u r -> p b r u"),
            )
            return target

        def quantise_weight(grouped, pair, codes, scales):
            columns = slice(pair * 2 * P, (pair + 1) * 2 * P)
            nc.vector.quantize_mx(
                out=codes[:, columns].bitcast(FP8X4), scales=scales[:, columns], in_=grouped
            )

        def project(n, chunk, piece, u_tiles):
            block, pd = divmod(piece, 2)
            channels = slice(block * P, (block + 1) * P)
            z = z_pool.tile([P, 2, PLANE], F32)
            for i in range(2):
                place = 2 * pd + i if n == 0 and chunk == 0 else 2 * i + pd
                plane = slice(chunk * CHUNK + place * PLANE, chunk * CHUNK + (place + 1) * PLANE)
                nc.tensor.matmul_mx(
                    out=z[:, i, :],
                    lhsT=w1_codes[:, channels].bitcast(FP8X4),
                    lhsT_scale=w1_scales[:, channels],
                    rhs=x_codes[n][:, plane].bitcast(FP8X4),
                    rhs_scale=x_scales[n][:, plane],
                    start=True,
                    stop=True,
                )
            if chunk == 0:
                u_tiles[n * PIECES + piece] = u_pool.tile([P, 4 * CELLS], BF16, name="u")
            nc.scalar.activation(
                out=u_tiles[n * PIECES + piece][:]
                .rearrange("c (q g) -> c q g", q=4)[:, :, chunk * P : (chunk + 1) * P]
                .rearrange("c q (a gw) -> c q a gw", gw=GRID),
                in_=z[:].rearrange("c i (gh q gw) -> c q (i gh) gw", q=4, gw=GRID),
                func=GELU,
                bias=b1_columns[:, block : block + 1],
                scale=1.0,
            )

        def mix(n, piece, ph, half, u_codes, u_scales, result):
            block, pd = divmod(piece, 2)
            result_view = result[:].rearrange(
                "c (gd gh ph gw pw) -> c ph gd gh gw pw", gd=GRID, gh=GRID, ph=2, gw=GRID, pw=2
            )
            cells = slice(half * HALF, (half + 1) * HALF)
            y = y_pool.tile([P, 2, HALF], F32)
            for pw in range(2):
                nc.tensor.matmul_mx(
                    out=y[:, pw, :],
                    lhsT=u_codes[:, pw * P : (pw + 1) * P].bitcast(FP8X4),
                    lhsT_scale=u_scales[:, pw * P : (pw + 1) * P],
                    rhs=w2_codes[:, cells].bitcast(FP8X4),
                    rhs_scale=w2_scales[:, cells],
                    start=True,
                    stop=True,
                )
            parts = 2 if (n, piece, ph, half) == (BATCH - 1, PIECES - 1, 1, 1) else 1
            for part in range(parts):
                gd = slice(4 * half + part * 4 // parts, 4 * half + (part + 1) * 4 // parts)
                nc.vector.tensor_tensor(
                    out=result_view[:, ph, gd],
                    in0=y[:].rearrange("c pw (gd gh gw) -> c gd gh gw pw", gd=4, gh=GRID)[
                        :, part * 4 // parts : (part + 1) * 4 // parts
                    ],
                    in1=b2_all[:]
                    .rearrange("c (gd gh gw) -> c gd gh gw", gd=GRID, gh=GRID)[:, gd]
                    .unsqueeze(4)
                    .to_broadcast([P, 4 // parts, GRID, GRID, 2]),
                    op=ADD,
                )
                if ph == 1:
                    nc.sync.dma_start(
                        out=out_planes[n, block * P : (block + 1) * P, pd, gd],
                        in_=result[:].rearrange("c (gd v) -> c gd v", gd=GRID)[:, gd],
                    )

        b1_rows = keep.tile([P, P], BF16)
        nc.vector.memset(b1_rows[:], 0.0)
        raw_slabs = [[], []]
        nc.sync.dma_start(out=b1_rows[0:BLOCKS, :], in_=b1_u.rearrange("(b r) -> b r", r=P))
        w1_rows = [load_weight(w1_u, 0)]
        raw_slabs[0].append(load_planes(0, 0))
        w1_rows.append(load_weight(w1_u, 1))
        raw_slabs[0].append(load_planes(0, 1))
        for chunk in range(1, CHUNKS):
            raw_slabs[0] += load_chunk(0, chunk)
        w2_rows = [load_weight(w2, pair) for pair in range(2)]
        b2_all = keep.tile([P, CELLS], BF16)
        nc.sync.dma_start(out=b2_all[:], in_=b2.partition_broadcast(P))
        for chunk in range(CHUNKS):
            raw_slabs[1] += load_chunk(1, chunk)

        b1_rows_f32 = keep.tile([P, P], F32)
        nc.vector.tensor_copy(out=b1_rows_f32[:], in_=b1_rows[:])
        b1_flipped = flipped_pool.tile([P, 2, 2, P], F32, tag="flipped")
        nc.tensor.transpose(b1_flipped[:, 0, 0, :], b1_rows_f32[:], identity[:])
        b1_columns = keep.tile([P, BLOCKS], F32)
        nc.vector.tensor_copy(out=b1_columns[:], in_=b1_flipped[:, 0, 0, 0:BLOCKS])
        u_tiles = {}
        w1_grouped = transpose_two_blocks(w1_rows[0][:], nc.scalar.copy)
        x_grouped = regroup_slab(raw_slabs[0][0], HEAD_SCALAR_ROWS, x_grouped_pool, nc.vector)
        quantise_weight(w1_grouped, 0, w1_codes, w1_scales)
        w1_grouped = transpose_two_blocks(w1_rows[1][:], nc.scalar.copy)
        quantise_slab(0, 0, x_grouped)
        x_grouped = regroup_slab(raw_slabs[0][1], SECOND_SCALAR_ROWS, x_grouped_pool, nc.vector)
        quantise_weight(w1_grouped, 1, w1_codes, w1_scales)
        for block in range(BLOCKS):
            project(0, 0, 2 * block, u_tiles)
        quantise_slab(0, 1, x_grouped)

        for chunk in range(1, CHUNKS):
            x_grouped = [regroup_slab(raw_slabs[0][2 * chunk + i], 0, x_grouped_pool, nc.vector) for i in range(2)]
            for i in range(2):
                quantise_slab(0, 2 * chunk + i, x_grouped[i])
            if chunk == 1:
                for block in range(BLOCKS):
                    project(0, 0, 2 * block + 1, u_tiles)
            if chunk == 2:
                for piece in range(PIECES):
                    project(0, 1, piece, u_tiles)
        for slab in range(EARLY_SLABS):
            x_grouped = regroup_slab(raw_slabs[1][slab], 0, x_grouped_pool, nc.vector)
            quantise_slab(1, slab, x_grouped)
        late = {EARLY_SLABS: regroup_slab(raw_slabs[1][EARLY_SLABS], 0, late_pool, nc.vector)}
        grouped_tiles = {}

        def flip(step):
            piece = grouped_pool.tile([P, CELLS * PACK], BF16, align_bytes=64)
            for ph in range(2):
                part = slice(2 * ph * CELLS, 2 * (ph + 1) * CELLS)
                transpose_two_blocks(u_tiles[step][:, part], nc.scalar.copy, piece[:, part])
            grouped_tiles[step] = piece

        project(0, 2, 0, u_tiles)
        w2_grouped = [transpose_two_blocks(w2_rows[pair][:], nc.scalar.copy) for pair in range(2)]
        project(0, 3, 0, u_tiles)
        project(0, 2, 1, u_tiles)
        flip(0)
        for pair in range(2):
            quantise_weight(w2_grouped[pair], pair, w2_codes, w2_scales)
        project(0, 3, 1, u_tiles)

        project_steps = {}
        for step in range(2, BATCH * PIECES):
            n, piece = divmod(step, PIECES)
            for chunk in range(HALF_CHUNKS, CHUNKS):
                if n or chunk > HALF_CHUNKS or piece >= 2:
                    project_steps.setdefault(step - 2, []).append((n, chunk, piece))
        for i in range(PIECES * HALF_CHUNKS):
            piece, chunk = divmod(i, HALF_CHUNKS)
            project_steps[FIRST_STEP + i * 3 // 4].append((1, chunk, piece))
        operands = {}
        for step in range(BATCH * PIECES + 1):
            projects = project_steps.get(step, [])
            n, piece = divmod(step - 1, PIECES)
            if step >= 1:
                result = result_pool.tile([P, VOXELS // 2], F32, name="result")
            if step >= 1:
                mix(n, piece, 0, 0, *operands[step - 1, 0], result)
            if step >= 1:
                mix(n, piece, 1, 0, *operands[step - 1, 1], result)
            if len(projects) > 2:
                project(*projects.pop(2), u_tiles)
            if step < BATCH * PIECES:
                u_codes = u_mx_pool.tile([P, CELLS], U32, align_bytes=64)
                u_scales = u_mx_pool.tile([P, CELLS], U8, align_bytes=64)
                nc.vector.quantize_mx(out=u_codes[:].bitcast(FP8X4), scales=u_scales[:], in_=grouped_tiles[step][:])
                for ph in range(2):
                    part = slice(ph * 2 * P, (ph + 1) * 2 * P)
                    operands[step, ph] = (u_codes[:, part], u_scales[:, part])
            slab = step + EARLY_SLABS
            if slab < SLABS:
                quantise_slab(1, slab, late[slab])
            if slab + 1 < SLABS:
                late[slab + 1] = regroup_slab(raw_slabs[1][slab + 1], LATE_SCALAR_ROWS, late_pool, nc.gpsimd, 12 if step == 0 else 0)
            if step >= 1:
                mix(n, piece, 0, 1, *operands[step - 1, 0], result)
            if projects:
                project(*projects.pop(0), u_tiles)
            if step + 1 < BATCH * PIECES:
                flip(step + 1)
            if step >= 1:
                mix(n, piece, 1, 1, *operands[step - 1, 1], result)
            if projects:
                project(*projects.pop(0), u_tiles)
            for bank in projects:
                project(*bank, u_tiles)
            if slab + 1 < SLABS:
                regroup_rest(raw_slabs[1][slab + 1], LATE_SCALAR_ROWS, late[slab + 1])
